import numpy as np
import ml_dtypes


def mxq(x, axis, fmt="e4m3"):
    dtype, down = {"e4m3": (ml_dtypes.float8_e4m3fn, 7), "e5m2": (ml_dtypes.float8_e5m2, 14)}[fmt]
    v = np.moveaxis(np.asarray(x, np.float32).astype(ml_dtypes.bfloat16).astype(np.float64), axis, -1)
    blocks = v.reshape(v.shape[:-1] + (-1, 32))
    amax = np.abs(blocks).max(-1, keepdims=True)
    byte = np.maximum(np.where(amax > 0, np.frexp(amax)[1] - 1 + 127, 0) - down, 1)
    scale = np.exp2(byte - 127.0)
    codes = (blocks / scale).astype(np.float32).astype(dtype).astype(np.float64)
    return np.moveaxis((codes * scale).reshape(v.shape), -1, axis)


WIDE = False


def mx_kscale(k):
    if not WIDE:
        return np.ones(k)
    levels = np.array([10, -10, 5, -5, 0])
    if k % 512:
        return np.exp2(np.random.permutation(np.resize(levels, k // 32))).repeat(32)
    a = np.empty((k // 512, 16))
    for p in range(k // 512):
        a[p, :8] = np.random.permutation(np.resize(levels, 8))
        for g in range(8):
            far = levels[np.abs(levels - a[p, g]) >= 10]
            a[p, g + 8] = far[np.random.randint(len(far))]
    return np.exp2(a.ravel()).repeat(32)


BF16 = ml_dtypes.bfloat16


def bf(x):
    return np.asarray(x, np.float32).astype(BF16)


def f64(x):
    return np.asarray(x).astype(np.float64)


B, C, T, H = 4, 1536, 512, 512
EPS_LN = 1e-5
EPS_STD = 1e-5


def ln_dim1(z, g, b):
    mu = z.mean(axis=1, keepdims=True)
    var = ((z - mu) ** 2).mean(axis=1, keepdims=True)
    return (z - mu) / np.sqrt(var + EPS_LN) * g[None, :, None] + b[None, :, None]


def stats(x, m):
    mean = (m * x).sum(axis=2)
    std = np.sqrt(np.maximum((m * x * x).sum(axis=2) - mean ** 2, EPS_STD))
    return mean, std


def setup_inputs():
    s = mx_kscale(C)
    lens = np.random.randint(T // 2, T, size=B)
    mask = (np.arange(T)[None, None, :] < lens[:, None, None]) * 1.0
    off = 0.5 * np.random.standard_normal((B, C, 1))
    gain = 0.5 + np.random.random((B, C, 1))
    pad = np.random.standard_normal((B, C, 1)) * (1.0 - mask)
    x = off + gain * np.random.standard_normal((B, C, T)) + pad
    return {"x": bf(x * s[None, :, None]),
            "mask": bf(mask),
            "w1": bf(np.random.standard_normal((H, 3 * C)) / np.sqrt(3 * C) / np.tile(s, 3)[None, :]),
            "b1": bf(0.1 * np.random.standard_normal(H)),
            "g1": bf(1.0 + 0.1 * np.random.standard_normal(H)),
            "be1": bf(0.1 * np.random.standard_normal(H))}


def reference(x, mask, w1, b1, g1, be1):
    x, mask = f64(x), f64(mask)
    total = mask.sum(axis=2, keepdims=True)
    mean0, std0 = stats(x, mask / total)
    mean0 = mean0
    std0 = std0
    x_in = np.concatenate([
        x,
        np.broadcast_to(mean0[:, :, None], (B, C, T)),
        np.broadcast_to(std0[:, :, None], (B, C, T)),
    ], axis=1)
    u = (mxq(f64(w1), 1, "e4m3") @ mxq(x_in, 1, "e4m3")) + f64(b1)[None, :, None]
    return np.tanh(ln_dim1(np.maximum(u, 0.0), f64(g1), f64(be1)))

@@ -1,0 +1,352 @@
+from contextlib import ExitStack
+
+import concourse.mybir as mybir
+from concourse.masks import make_identity
+
+F32 = mybir.dt.float32
+BF16 = mybir.dt.bfloat16
+U32 = mybir.dt.uint32
+U8 = mybir.dt.uint8
+FP8X4 = mybir.dt.float8_e4m3fn_x4
+ALU = mybir.AluOpType
+ACT = mybir.ActivationFunctionType
+AX = mybir.AxisListType
+
+B, C, T, H = 4, 1536, 512, 512
+P = 128
+SLOTS = 4
+K_PASS = P * SLOTS
+X_PASSES = C // K_PASS
+W_PASSES = 3 * X_PASSES
+ROWS = X_PASSES * SLOTS
+H_TILES = H // P
+T_TILES = T // P
+STAT_STEP = 64
+EPS_LN = 1e-5
+EPS_STD = 1e-5
+FLOPS = 2 * B * H * 3 * C * T
+
+
+def tile_attentivestatspool_pa_kernel(tc, x, mask, w1, b1, g1, be1, out):
+    nc = tc.nc
+    with ExitStack() as ctx:
+        const = ctx.enter_context(tc.tile_pool(name="const", bufs=1))
+        loads = ctx.enter_context(tc.tile_pool(name="loads", bufs=5))
+        three = ctx.enter_context(tc.tile_pool(name="three", bufs=3))
+        four = ctx.enter_context(tc.tile_pool(name="four", bufs=4))
+        two = ctx.enter_context(tc.tile_pool(name="two", bufs=2))
+        ps_first = ctx.enter_context(tc.psum_pool(name="ps_first", bufs=4))
+        ps_mx = ctx.enter_context(tc.psum_pool(name="ps_mx", bufs=2))
+        ps_back = ctx.enter_context(tc.psum_pool(name="ps_back", bufs=2))
+
+        mask_row = const.tile([P, B * T], BF16)
+        nc.vector.memset(mask_row[:], 0.0)
+        nc.sync.dma_start(out=mask_row[0:1, :], in_=mask.rearrange("b o t -> o (b t)"))
+        ones = const.tile([P, P], BF16)
+        nc.vector.memset(ones[:], 1.0)
+        mask_all = const.tile([P, B, T], BF16)
+        mask_sum = const.tile([P, B], F32)
+        param_rows = const.tile([P, P], BF16)
+        nc.vector.memset(param_rows[:], 0.0)
+        warm = const.tile([P, 1], F32)
+        nc.vector.memset(warm[:], 0.0)
+        nc.scalar.activation(out=warm[:], in_=warm[:], func=ACT.Tanh)
+
+        def load_x(b):
+            x_tile = loads.tile([P, ROWS, T], BF16, tag="load", name="x_tile%d" % b)
+            for g in range(X_PASSES):
+                nc.sync.dma_start(
+                    out=x_tile[:, SLOTS * g : SLOTS * (g + 1), :],
+                    in_=x[b, K_PASS * g : K_PASS * (g + 1), :].rearrange(
+                        "(p j) t -> p j t", j=SLOTS
+                    ),
+                )
+            return x_tile
+
+        def load_w(third):
+            w_tile = loads.tile([P, H_TILES, C], BF16, tag="load", name="w_tile%d" % third)
+            nc.sync.dma_start(
+                out=w_tile[:],
+                in_=w1[:, C * third : C * (third + 1)].rearrange("(a p) k -> p a k", p=P),
+            )
+            return w_tile
+
+        x_tiles = [load_x(0)]
+        w_tiles = [load_w(third) for third in range(3)]
+        x_tiles.append(load_x(1))
+        nc.sync.dma_start(out=param_rows[0:4, :], in_=b1.rearrange("(r c) -> r c", c=P))
+        nc.sync.dma_start(out=param_rows[4:8, :], in_=g1.rearrange("(r c) -> r c", c=P))
+        nc.sync.dma_start(out=param_rows[8:12, :], in_=be1.rearrange("(r c) -> r c", c=P))
+
+        ident_f32 = const.tile([P, P], F32)
+        make_identity(nc, ident_f32[:])
+        ident_bf16 = const.tile([P, P], BF16)
+        make_identity(nc, ident_bf16[:])
+        stat_in = const.tile([P, 8, STAT_STEP, SLOTS], BF16, align_bytes=64)
+        nc.vector.memset(stat_in[:], 0.0)
+        half = const.tile([P, ROWS], F32)
+        nc.vector.memset(half[:], 0.5)
+        minus_half = const.tile([P, 4], F32)
+        nc.vector.memset(minus_half[:], -0.5)
+
+        w_codes = const.tile([P, W_PASSES, H], U32, align_bytes=64)
+        w_scales = const.tile([P, W_PASSES, H], U8, align_bytes=64)
+
+        for b in range(B):
+            mask_ps = ps_mx.tile([P, T], F32, tag="mx")
+            nc.tensor.matmul(
+                out=mask_ps[:], lhsT=ones[:], rhs=mask_row[:, T * b : T * (b + 1)],
+                start=True, stop=True,
+            )
+            nc.scalar.activation(
+                out=mask_all[:, b, :], in_=mask_ps[:], func=ACT.Copy,
+                accum_out=mask_sum[:, b : b + 1],
+            )
+        inv_sum = const.tile([P, B], F32)
+        inv_sum_256 = const.tile([P, B], F32)
+        params = const.tile([P, 12], F32)
+
+        stats = {}
+        x_grouped = {}
+        x_quant = {}
+        w_grouped = {}
+        stat_ps = {}
+        relu_out = {}
+
+        def masked_stats(b, g):
+            if g == 0:
+                stats_b = two.tile([P, ROWS, 6], F32, tag="stats")
+                stats[b] = stats_b
+            x_masked = two.tile([P, SLOTS, T], BF16, tag="x_masked")
+            nc.vector.tensor_tensor(
+                out=x_masked[:],
+                in0=x_tiles[b][:, SLOTS * g : SLOTS * (g + 1), :],
+                in1=mask_all[:, b, :].unsqueeze(1).to_broadcast([P, SLOTS, T]),
+                op=ALU.mult,
+            )
+            for j in range(SLOTS):
+                nc.vector.bn_stats(out=stats[b][:, SLOTS * g + j, :], in_=x_masked[:, j, :])
+
+        def transpose_w(g):
+            third, g_in = divmod(g, X_PASSES)
+            w_words = w_tiles[third][:].bitcast(F32)
+            w_group = four.tile([P, H, SLOTS], BF16, tag="w_group", align_bytes=64)
+            w_grouped[g] = w_group
+            group_words = w_group[:].bitcast(F32)
+            for pair in range(2):
+                w_ps = ps_first.tile([P, 2, 2 * P], F32, tag="first")
+                for u in range(2):
+                    for a in range(2):
+                        first_word = 2 * P * g_in + u
+                        nc.tensor.transpose(
+                            w_ps[:, u, P * a : P * (a + 1)],
+                            w_words[:, 2 * pair + a, first_word : first_word + 2 * P - 1 : 2],
+                            ident_f32[:],
+                        )
+                nc.scalar.copy(
+                    out=group_words[:, 2 * P * pair : 2 * P * (pair + 1), :],
+                    in_=w_ps[:].rearrange("p u n -> p n u"),
+                )
+
+        def quantise_w(g):
+            nc.vector.quantize_mx(
+                out=w_codes[:, g, :].bitcast(FP8X4),
+                scales=w_scales[:, g, :],
+                in_=w_grouped[g][:].rearrange("p h j -> p (h j)"),
+            )
+
+        def group_x(b, g):
+            x_group = three.tile([P, T, SLOTS], BF16, tag="x_group", align_bytes=64)
+            x_grouped[(b, g)] = x_group
+            nc.scalar.copy(
+                out=x_group[:].rearrange("p (c i) j -> p c j i", i=4),
+                in_=x_tiles[b][:, SLOTS * g : SLOTS * (g + 1), :].rearrange(
+                    "p j (c i) -> p c j i", i=4
+                ),
+            )
+
+        def quantise_x(b, g):
+            if g == 0:
+                x_codes = three.tile([P, X_PASSES, T], U32, tag="x_codes", align_bytes=64)
+                x_scales = three.tile([P, X_PASSES, T], U8, tag="x_scales", align_bytes=64)
+                x_quant[b] = (x_codes, x_scales)
+            x_codes, x_scales = x_quant[b]
+            nc.vector.quantize_mx(
+                out=x_codes[:, g, :].bitcast(FP8X4),
+                scales=x_scales[:, g, :],
+                in_=x_grouped[(b, g)][:].rearrange("p t j -> p (t j)"),
+            )
+
+        def mean_and_std(b):
+            halves = stats[b][:].rearrange("p r (h s) -> p (r h) s", s=3)
+            half_mean = halves[:, :, 1]
+            half_dev = halves[:, :, 2]
+            mean_sq = two.tile([P, 2 * ROWS], F32, tag="mean_sq")
+            nc.vector.tensor_tensor(out=mean_sq[:], in0=half_mean, in1=half_mean, op=ALU.mult)
+            half_sq = two.tile([P, 2 * ROWS], F32, tag="half_sq")
+            nc.vector.scalar_tensor_tensor(
+                out=half_sq[:], in0=mean_sq[:], scalar=256.0, in1=half_dev,
+                op0=ALU.mult, op1=ALU.add,
+            )
+            sum_sq = two.tile([P, ROWS], F32, tag="sum_sq")
+            nc.vector.tensor_reduce(
+                out=sum_sq[:], in_=half_sq[:].rearrange("p (r h) -> p r h", h=2),
+                axis=AX.X, op=ALU.add,
+            )
+            sum_mean = two.tile([P, ROWS], F32, tag="sum_mean")
+            nc.vector.tensor_reduce(
+                out=sum_mean[:], in_=half_mean.rearrange("p (r h) -> p r h", h=2),
+                axis=AX.X, op=ALU.add,
+            )
+            mean0 = two.tile([P, ROWS], F32, tag="mean0")
+            nc.vector.tensor_scalar_mul(
+                out=mean0[:], in0=sum_mean[:], scalar1=inv_sum_256[:, b : b + 1]
+            )
+            mean0_sq = two.tile([P, ROWS], F32, tag="mean0_sq")
+            nc.vector.tensor_tensor(out=mean0_sq[:], in0=mean0[:], in1=mean0[:], op=ALU.mult)
+            var0 = two.tile([P, ROWS], F32, tag="var0")
+            nc.vector.scalar_tensor_tensor(
+                out=var0[:], in0=sum_sq[:], scalar=inv_sum[:, b : b + 1], in1=mean0_sq[:],
+                op0=ALU.mult, op1=ALU.subtract,
+            )
+            var0_floor = two.tile([P, ROWS], F32, tag="var0_floor")
+            nc.vector.tensor_scalar_max(out=var0_floor[:], in0=var0[:], scalar1=EPS_STD)
+            nc.gpsimd.tensor_tensor(
+                out=stat_in[:, X_PASSES : 2 * X_PASSES, b, :],
+                in0=var0_floor[:].rearrange("p (g j) -> p g j", j=SLOTS),
+                in1=half[:].rearrange("p (g j) -> p g j", j=SLOTS),
+                op=ALU.pow,
+            )
+            nc.vector.tensor_copy(
+                out=stat_in[:, 0:X_PASSES, b, :],
+                in_=mean0[:].rearrange("p (g j) -> p g j", j=SLOTS),
+            )
+
+        def stat_product(b):
+            stat_codes = two.tile([P, 8 * STAT_STEP], U32, tag="stat_codes", align_bytes=64)
+            stat_scales = two.tile([P, 8 * STAT_STEP], U8, tag="stat_scales", align_bytes=64)
+            nc.vector.quantize_mx(
+                out=stat_codes[:].bitcast(FP8X4),
+                scales=stat_scales[:],
+                in_=stat_in[:].rearrange("p s n j -> p (s n j)"),
+            )
+            product = ps_mx.tile([P, H_TILES, P], F32, tag="mx")
+            stat_ps[b] = product
+            for ht in range(H_TILES):
+                for s in range(2 * X_PASSES):
+                    nc.tensor.matmul_mx(
+                        out=product[:, ht, :],
+                        lhsT=w_codes[:, X_PASSES + s, P * ht : P * (ht + 1)].bitcast(FP8X4),
+                        lhsT_scale=w_scales[:, X_PASSES + s, P * ht : P * (ht + 1)],
+                        rhs=stat_codes[:, STAT_STEP * s : STAT_STEP * s + P].bitcast(FP8X4),
+                        rhs_scale=stat_scales[:, STAT_STEP * s : STAT_STEP * s + P],
+                        start=(s == 0),
+                        stop=(s == 2 * X_PASSES - 1),
+                    )
+
+        def main_product(b):
+            bias = two.tile([P, H_TILES], F32, tag="bias")
+            nc.vector.tensor_tensor(
+                out=bias[:], in0=stat_ps[b][:, :, b], in1=params[:, 0:4], op=ALU.add
+            )
+            x_codes, x_scales = x_quant[b]
+            u = three.tile([P, H_TILES, T], F32, tag="u")
+            relu_out[b] = u
+            for ht in range(H_TILES):
+                acc = ps_mx.tile([P, T], F32, tag="mx")
+                for g in range(X_PASSES):
+                    nc.tensor.matmul_mx(
+                        out=acc[:],
+                        lhsT=w_codes[:, g, P * ht : P * (ht + 1)].bitcast(FP8X4),
+                        lhsT_scale=w_scales[:, g, P * ht : P * (ht + 1)],
+                        rhs=x_codes[:, g, :].bitcast(FP8X4),
+                        rhs_scale=x_scales[:, g, :],
+                        start=(g == 0),
+                        stop=(g == X_PASSES - 1),
+                    )
+                nc.scalar.activation(
+                    out=u[:, ht, :], in_=acc[:], func=ACT.Relu, bias=bias[:, ht : ht + 1], scale=1.0
+                )
+
+        def layer_norm(b):
+            u = relu_out[b]
+            normed = two.tile([P, T_TILES, H], F32, tag="normed")
+            for pair in range(2):
+                ln_stats = four.tile([P, 2, 6], F32, tag="ln_stats")
+                mean_var = four.tile([P, 2, 2], F32, tag="mean_var")
+                banks = []
+                for i in range(2):
+                    tb = 2 * pair + i
+                    u_t = ps_first.tile([P, H], F32, tag="first")
+                    for ht in range(H_TILES):
+                        nc.tensor.transpose(
+                            u_t[:, P * ht : P * (ht + 1)], u[:, ht, P * tb : P * (tb + 1)],
+                            ident_f32[:],
+                        )
+                    nc.vector.bn_stats(out=ln_stats[:, i, :], in_=u_t[:])
+                    nc.vector.bn_aggr(out=mean_var[:, i, :], in_=ln_stats[:, i, :])
+                    banks.append(u_t)
+                var_eps = four.tile([P, 2], F32, tag="var_eps")
+                nc.vector.tensor_scalar_add(out=var_eps[:], in0=mean_var[:, :, 1], scalar1=EPS_LN)
+                neg_mean = four.tile([P, 2], F32, tag="neg_mean")
+                nc.vector.tensor_scalar_mul(out=neg_mean[:], in0=mean_var[:, :, 0], scalar1=-1.0)
+                rstd = four.tile([P, 2], F32, tag="rstd")
+                nc.gpsimd.tensor_tensor(
+                    out=rstd[:], in0=var_eps[:], in1=minus_half[:, 0:2], op=ALU.pow
+                )
+                shift = four.tile([P, 2], F32, tag="shift")
+                nc.gpsimd.tensor_tensor(out=shift[:], in0=neg_mean[:], in1=rstd[:], op=ALU.mult)
+                for i in range(2):
+                    nc.scalar.activation(
+                        out=normed[:, 2 * pair + i, :], in_=banks[i][:], func=ACT.Identity,
+                        scale=rstd[:, i : i + 1], bias=shift[:, i : i + 1],
+                    )
+            for ht in range(H_TILES):
+                back = ps_back.tile([P, T], F32, tag="back")
+                for tb in range(T_TILES):
+                    nc.tensor.transpose(
+                        back[:, P * tb : P * (tb + 1)], normed[:, tb, P * ht : P * (ht + 1)],
+                        ident_f32[:],
+                    )
+                result = four.tile([P, T], F32, tag="result")
+                nc.scalar.activation(
+                    out=result[:], in_=back[:], func=ACT.Tanh,
+                    scale=params[:, 4 + ht : 5 + ht], bias=params[:, 8 + ht : 9 + ht],
+                )
+                nc.sync.dma_start(out=out[b, P * ht : P * (ht + 1), :], in_=result[:])
+
+        for g in range(X_PASSES):
+            group_x(0, g)
+            masked_stats(0, g)
+        x_tiles.append(load_x(2))
+        nc.vector.reciprocal(out=inv_sum[:], in_=mask_sum[:])
+        nc.vector.tensor_scalar_mul(out=inv_sum_256[:], in0=inv_sum[:], scalar1=256.0)
+        mean_and_std(0)
+        for g in range(W_PASSES):
+            transpose_w(g)
+            quantise_w(g)
+            if g == X_PASSES - 1:
+                x_tiles.append(load_x(3))
+        for g in range(X_PASSES):
+            quantise_x(0, g)
+        param_ps = ps_mx.tile([P, P], BF16, tag="mx")
+        nc.tensor.transpose(param_ps[:], param_rows[:], ident_bf16[:])
+        nc.vector.tensor_copy(out=params[:], in_=param_ps[:, 0:12])
+        stat_product(0)
+        main_product(0)
+        for b in range(1, B):
+            for g in range(X_PASSES):
+                group_x(b, g)
+                masked_stats(b, g)
+                if b == 3 and g == 0:
+                    layer_norm(1)
+            if b == 2:
+                layer_norm(0)
+            mean_and_std(b)
+            for g in range(X_PASSES):
+                quantise_x(b, g)
+            stat_product(b)
+            if b == 3:
+                layer_norm(2)
+            main_product(b)
+        layer_norm(3)

@@ -31,26 +31,36 @@ def tile_attentivestatspool_pa_kernel(tc, x, mask, w1, b1, g1, be1, out):
     nc = tc.nc
     with ExitStack() as ctx:
         const = ctx.enter_context(tc.tile_pool(name="const", bufs=1))
-        loads = ctx.enter_context(tc.tile_pool(name="loads", bufs=5))
-        three = ctx.enter_context(tc.tile_pool(name="three", bufs=3))
+        loads = ctx.enter_context(tc.tile_pool(name="loads", bufs=6))
+        five = ctx.enter_context(tc.tile_pool(name="five", bufs=5))
         four = ctx.enter_context(tc.tile_pool(name="four", bufs=4))
         two = ctx.enter_context(tc.tile_pool(name="two", bufs=2))
         ps_first = ctx.enter_context(tc.psum_pool(name="ps_first", bufs=4))
-        ps_mx = ctx.enter_context(tc.psum_pool(name="ps_mx", bufs=2))
-        ps_back = ctx.enter_context(tc.psum_pool(name="ps_back", bufs=2))
+        ps_mx = ctx.enter_context(tc.psum_pool(name="ps_mx", bufs=4))
+        ctx.enter_context(
+            tc.manual_schedule(
+                engines={
+                    mybir.EngineType.DVE, mybir.EngineType.Activation,
+                    mybir.EngineType.PE, mybir.EngineType.Pool,
+                }
+            )
+        )
 
         mask_row = const.tile([P, B * T], BF16)
-        nc.vector.memset(mask_row[:], 0.0)
-        nc.sync.dma_start(out=mask_row[0:1, :], in_=mask.rearrange("b o t -> o (b t)"))
+        mask_words = mask_row[:].bitcast(F32)
+        nc.vector.memset(mask_words[:, 0 : T // 2], 0.0)
+        nc.gpsimd.memset(mask_words[:, T // 2 : B * T // 2], 0.0)
+        mask_flat = mask.rearrange("b o t -> o (b t)")
+        nc.sync.dma_start(out=mask_row[0:1, 0:T], in_=mask_flat[:, 0:T])
         ones = const.tile([P, P], BF16)
         nc.vector.memset(ones[:], 1.0)
         mask_all = const.tile([P, B, T], BF16)
         mask_sum = const.tile([P, B], F32)
-        param_rows = const.tile([P, P], BF16)
-        nc.vector.memset(param_rows[:], 0.0)
         warm = const.tile([P, 1], F32)
-        nc.vector.memset(warm[:], 0.0)
-        nc.scalar.activation(out=warm[:], in_=warm[:], func=ACT.Tanh)
+        nc.vector.memset(warm[:], 1.0)
+        nc.scalar.activation(out=warm[:], in_=warm[:], func=ACT.Sqrt)
+        param_rows = const.tile([P, P], BF16)
+        nc.gpsimd.memset(param_rows[:], 0.0)
 
         def load_x(b):
             x_tile = loads.tile([P, ROWS, T], BF16, tag="load", name="x_tile%d" % b)
@@ -72,65 +82,87 @@ def tile_attentivestatspool_pa_kernel(tc, x, mask, w1, b1, g1, be1, out):
             return w_tile
 
         x_tiles = [load_x(0)]
+        nc.sync.dma_start(out=mask_row[0:1, T : B * T], in_=mask_flat[:, T : B * T])
         w_tiles = [load_w(third) for third in range(3)]
         x_tiles.append(load_x(1))
         nc.sync.dma_start(out=param_rows[0:4, :], in_=b1.rearrange("(r c) -> r c", c=P))
         nc.sync.dma_start(out=param_rows[4:8, :], in_=g1.rearrange("(r c) -> r c", c=P))
         nc.sync.dma_start(out=param_rows[8:12, :], in_=be1.rearrange("(r c) -> r c", c=P))
+        x_tiles.append(load_x(2))
+        x_tiles.append(load_x(3))
 
         ident_f32 = const.tile([P, P], F32)
         make_identity(nc, ident_f32[:])
         ident_bf16 = const.tile([P, P], BF16)
         make_identity(nc, ident_bf16[:])
         stat_in = const.tile([P, 8, STAT_STEP, SLOTS], BF16, align_bytes=64)
-        nc.vector.memset(stat_in[:], 0.0)
-        half = const.tile([P, ROWS], F32)
-        nc.vector.memset(half[:], 0.5)
+        nc.gpsimd.memset(stat_in[:].rearrange("p s n j -> p (s n j)").bitcast(F32), 0.0)
+        half = const.tile([P, X_PASSES, SLOTS], F32)
+        nc.gpsimd.memset(half[:], 0.5)
         minus_half = const.tile([P, 4], F32)
-        nc.vector.memset(minus_half[:], -0.5)
+        nc.gpsimd.memset(minus_half[:], -0.5)
 
         w_codes = const.tile([P, W_PASSES, H], U32, align_bytes=64)
         w_scales = const.tile([P, W_PASSES, H], U8, align_bytes=64)
 
-        for b in range(B):
+        def spread_mask(b):
             mask_ps = ps_mx.tile([P, T], F32, tag="mx")
             nc.tensor.matmul(
                 out=mask_ps[:], lhsT=ones[:], rhs=mask_row[:, T * b : T * (b + 1)],
                 start=True, stop=True,
             )
-            nc.scalar.activation(
-                out=mask_all[:, b, :], in_=mask_ps[:], func=ACT.Copy,
-                accum_out=mask_sum[:, b : b + 1],
-            )
+            if b == 0:
+                nc.vector.tensor_scalar(
+                    out=mask_all[:, b, :], in0=mask_ps[:], scalar1=1.0, scalar2=0.0,
+                    op0=ALU.mult, op1=ALU.add, accum_out=mask_sum[:, b : b + 1],
+                )
+            else:
+                nc.scalar.activation(
+                    out=mask_all[:, b, :], in_=mask_ps[:], func=ACT.Copy,
+                    accum_out=mask_sum[:, b : b + 1],
+                )
         inv_sum = const.tile([P, B], F32)
         inv_sum_256 = const.tile([P, B], F32)
         params = const.tile([P, 12], F32)
 
+        masked = {}
         stats = {}
+        moments = {}
+        sums = {}
         x_grouped = {}
         x_quant = {}
         w_grouped = {}
+        stat_quant = {}
         stat_ps = {}
+        main_ps = {}
+        results = {}
+        biases = {}
         relu_out = {}
+        u_banks = {}
+        scales = {}
+        normed_out = {}
 
-        def masked_stats(b, g):
-            if g == 0:
-                stats_b = two.tile([P, ROWS, 6], F32, tag="stats")
-                stats[b] = stats_b
+        def mask_x(b, g):
             x_masked = two.tile([P, SLOTS, T], BF16, tag="x_masked")
+            masked[(b, g)] = x_masked
             nc.vector.tensor_tensor(
                 out=x_masked[:],
                 in0=x_tiles[b][:, SLOTS * g : SLOTS * (g + 1), :],
                 in1=mask_all[:, b, :].unsqueeze(1).to_broadcast([P, SLOTS, T]),
                 op=ALU.mult,
             )
-            for j in range(SLOTS):
-                nc.vector.bn_stats(out=stats[b][:, SLOTS * g + j, :], in_=x_masked[:, j, :])
+
+        def channel_stats(b, g, slots):
+            if (b, g) not in stats:
+                stats_bg = four.tile([P, SLOTS, 6], F32, tag="stats")
+                stats[(b, g)] = stats_bg
+            for j in slots:
+                nc.vector.bn_stats(out=stats[(b, g)][:, j, :], in_=masked[(b, g)][:, j, :])
 
         def transpose_w(g):
             third, g_in = divmod(g, X_PASSES)
             w_words = w_tiles[third][:].bitcast(F32)
-            w_group = four.tile([P, H, SLOTS], BF16, tag="w_group", align_bytes=64)
+            w_group = five.tile([P, H, SLOTS], BF16, tag="w_group", align_bytes=64)
             w_grouped[g] = w_group
             group_words = w_group[:].bitcast(F32)
             for pair in range(2):
@@ -156,7 +188,7 @@ def tile_attentivestatspool_pa_kernel(tc, x, mask, w1, b1, g1, be1, out):
             )
 
         def group_x(b, g):
-            x_group = three.tile([P, T, SLOTS], BF16, tag="x_group", align_bytes=64)
+            x_group = four.tile([P, T, SLOTS], BF16, tag="x_group", align_bytes=64)
             x_grouped[(b, g)] = x_group
             nc.scalar.copy(
                 out=x_group[:].rearrange("p (c i) j -> p c j i", i=4),
@@ -167,8 +199,8 @@ def tile_attentivestatspool_pa_kernel(tc, x, mask, w1, b1, g1, be1, out):
 
         def quantise_x(b, g):
             if g == 0:
-                x_codes = three.tile([P, X_PASSES, T], U32, tag="x_codes", align_bytes=64)
-                x_scales = three.tile([P, X_PASSES, T], U8, tag="x_scales", align_bytes=64)
+                x_codes = two.tile([P, X_PASSES, T], U32, tag="x_codes", align_bytes=64)
+                x_scales = two.tile([P, X_PASSES, T], U8, tag="x_scales", align_bytes=64)
                 x_quant[b] = (x_codes, x_scales)
             x_codes, x_scales = x_quant[b]
             nc.vector.quantize_mx(
@@ -177,52 +209,75 @@ def tile_attentivestatspool_pa_kernel(tc, x, mask, w1, b1, g1, be1, out):
                 in_=x_grouped[(b, g)][:].rearrange("p t j -> p (t j)"),
             )
 
-        def mean_and_std(b):
-            halves = stats[b][:].rearrange("p r (h s) -> p (r h) s", s=3)
-            half_mean = halves[:, :, 1]
-            half_dev = halves[:, :, 2]
-            mean_sq = two.tile([P, 2 * ROWS], F32, tag="mean_sq")
-            nc.vector.tensor_tensor(out=mean_sq[:], in0=half_mean, in1=half_mean, op=ALU.mult)
-            half_sq = two.tile([P, 2 * ROWS], F32, tag="half_sq")
-            nc.vector.scalar_tensor_tensor(
-                out=half_sq[:], in0=mean_sq[:], scalar=256.0, in1=half_dev,
+        def channel_sums(b, g, engine):
+            if g == 0:
+                sum_x = two.tile([P, X_PASSES, SLOTS], F32, tag="sum_x")
+                sum_sq = two.tile([P, X_PASSES, SLOTS], F32, tag="sum_sq")
+                sums[b] = (sum_x, sum_sq)
+            sum_x, sum_sq = sums[b]
+            halves = stats[(b, g)][:].rearrange("p j (h s) -> p j h s", s=3)
+            mean_sq = two.tile([P, SLOTS, 2], F32, tag="mean_sq")
+            engine.tensor_tensor(
+                out=mean_sq[:], in0=halves[:, :, :, 1], in1=halves[:, :, :, 1], op=ALU.mult
+            )
+            dev = two.tile([P, SLOTS, 2], F32, tag="dev")
+            engine.tensor_scalar(
+                out=dev[:], in0=halves[:, :, :, 2], scalar1=1.0 / 256.0, scalar2=0.0,
                 op0=ALU.mult, op1=ALU.add,
             )
-            sum_sq = two.tile([P, ROWS], F32, tag="sum_sq")
-            nc.vector.tensor_reduce(
-                out=sum_sq[:], in_=half_sq[:].rearrange("p (r h) -> p r h", h=2),
-                axis=AX.X, op=ALU.add,
+            engine.tensor_tensor(
+                out=sum_x[:, g, :], in0=halves[:, :, 0, 1], in1=halves[:, :, 1, 1], op=ALU.add
             )
-            sum_mean = two.tile([P, ROWS], F32, tag="sum_mean")
-            nc.vector.tensor_reduce(
-                out=sum_mean[:], in_=half_mean.rearrange("p (r h) -> p r h", h=2),
-                axis=AX.X, op=ALU.add,
-            )
-            mean0 = two.tile([P, ROWS], F32, tag="mean0")
-            nc.vector.tensor_scalar_mul(
-                out=mean0[:], in0=sum_mean[:], scalar1=inv_sum_256[:, b : b + 1]
-            )
-            mean0_sq = two.tile([P, ROWS], F32, tag="mean0_sq")
-            nc.vector.tensor_tensor(out=mean0_sq[:], in0=mean0[:], in1=mean0[:], op=ALU.mult)
-            var0 = two.tile([P, ROWS], F32, tag="var0")
-            nc.vector.scalar_tensor_tensor(
-                out=var0[:], in0=sum_sq[:], scalar=inv_sum[:, b : b + 1], in1=mean0_sq[:],
-                op0=ALU.mult, op1=ALU.subtract,
-            )
-            var0_floor = two.tile([P, ROWS], F32, tag="var0_floor")
-            nc.vector.tensor_scalar_max(out=var0_floor[:], in0=var0[:], scalar1=EPS_STD)
-            nc.gpsimd.tensor_tensor(
-                out=stat_in[:, X_PASSES : 2 * X_PASSES, b, :],
-                in0=var0_floor[:].rearrange("p (g j) -> p g j", j=SLOTS),
-                in1=half[:].rearrange("p (g j) -> p g j", j=SLOTS),
-                op=ALU.pow,
-            )
-            nc.vector.tensor_copy(
-                out=stat_in[:, 0:X_PASSES, b, :],
-                in_=mean0[:].rearrange("p (g j) -> p g j", j=SLOTS),
+            half_sq = two.tile([P, SLOTS, 2], F32, tag="half_sq")
+            engine.tensor_tensor(out=half_sq[:], in0=mean_sq[:], in1=dev[:], op=ALU.add)
+            engine.tensor_tensor(
+                out=sum_sq[:, g, :], in0=half_sq[:, :, 0], in1=half_sq[:, :, 1], op=ALU.add
             )
 
-        def stat_product(b):
+        def invert_mask_sum(b):
+            nc.vector.reciprocal(out=inv_sum[:, b : b + 1], in_=mask_sum[:, b : b + 1])
+            nc.vector.tensor_scalar_mul(
+                out=inv_sum_256[:, b : b + 1], in0=inv_sum[:, b : b + 1], scalar1=256.0
+            )
+
+        def mean_and_var(b, groups, engine):
+            if groups.start == 0:
+                mean0 = two.tile([P, X_PASSES, SLOTS], F32, tag="mean0")
+                var0 = two.tile([P, X_PASSES, SLOTS], F32, tag="var0")
+                moments[b] = (mean0, var0)
+            mean0, var0 = moments[b]
+            gs = slice(groups.start, groups.stop)
+            sum_x, sum_sq = sums[b]
+            scale = inv_sum_256[:, b : b + 1]
+            engine.tensor_scalar_mul(out=mean0[:, gs, :], in0=sum_x[:, gs, :], scalar1=scale)
+            mean0_sq = two.tile([P, X_PASSES, SLOTS], F32, tag="mean0_sq")
+            engine.tensor_tensor(
+                out=mean0_sq[:, gs, :], in0=mean0[:, gs, :], in1=mean0[:, gs, :], op=ALU.mult
+            )
+            mean_sq0 = two.tile([P, X_PASSES, SLOTS], F32, tag="mean_sq0")
+            engine.tensor_scalar_mul(out=mean_sq0[:, gs, :], in0=sum_sq[:, gs, :], scalar1=scale)
+            diff = two.tile([P, X_PASSES, SLOTS], F32, tag="diff")
+            engine.tensor_tensor(
+                out=diff[:, gs, :], in0=mean_sq0[:, gs, :], in1=mean0_sq[:, gs, :],
+                op=ALU.subtract,
+            )
+            engine.tensor_scalar_max(out=var0[:, gs, :], in0=diff[:, gs, :], scalar1=EPS_STD)
+            engine.tensor_copy(out=stat_in[:, gs, b, :], in_=mean0[:, gs, :])
+
+        def square_root(b):
+            nc.scalar.activation(
+                out=stat_in[:, X_PASSES : 2 * X_PASSES, b, :], in_=moments[b][1][:], func=ACT.Sqrt
+            )
+
+        def power_root(b, groups):
+            gs = slice(groups.start, groups.stop)
+            n = len(groups)
+            nc.gpsimd.tensor_tensor(
+                out=stat_in[:, X_PASSES + groups.start : X_PASSES + groups.stop, b, :],
+                in0=moments[b][1][:, gs, :], in1=half[:, 0:n, :], op=ALU.pow,
+            )
+
+        def quantise_stats(b):
             stat_codes = two.tile([P, 8 * STAT_STEP], U32, tag="stat_codes", align_bytes=64)
             stat_scales = two.tile([P, 8 * STAT_STEP], U8, tag="stat_scales", align_bytes=64)
             nc.vector.quantize_mx(
@@ -230,6 +285,10 @@ def tile_attentivestatspool_pa_kernel(tc, x, mask, w1, b1, g1, be1, out):
                 scales=stat_scales[:],
                 in_=stat_in[:].rearrange("p s n j -> p (s n j)"),
             )
+            stat_quant[b] = (stat_codes, stat_scales)
+
+        def stat_product(b):
+            stat_codes, stat_scales = stat_quant[b]
             product = ps_mx.tile([P, H_TILES, P], F32, tag="mx")
             stat_ps[b] = product
             for ht in range(H_TILES):
@@ -244,16 +303,13 @@ def tile_attentivestatspool_pa_kernel(tc, x, mask, w1, b1, g1, be1, out):
                         stop=(s == 2 * X_PASSES - 1),
                     )
 
-        def main_product(b):
-            bias = two.tile([P, H_TILES], F32, tag="bias")
-            nc.vector.tensor_tensor(
-                out=bias[:], in0=stat_ps[b][:, :, b], in1=params[:, 0:4], op=ALU.add
-            )
+        def main_product(b, h_tiles):
             x_codes, x_scales = x_quant[b]
-            u = three.tile([P, H_TILES, T], F32, tag="u")
-            relu_out[b] = u
-            for ht in range(H_TILES):
+            if 0 in h_tiles:
+                main_ps[b] = []
+            for ht in h_tiles:
                 acc = ps_mx.tile([P, T], F32, tag="mx")
+                main_ps[b].append(acc)
                 for g in range(X_PASSES):
                     nc.tensor.matmul_mx(
                         out=acc[:],
@@ -264,89 +320,225 @@ def tile_attentivestatspool_pa_kernel(tc, x, mask, w1, b1, g1, be1, out):
                         start=(g == 0),
                         stop=(g == X_PASSES - 1),
                     )
+
+        def add_bias(b):
+            bias = two.tile([P, H_TILES], F32, tag="bias")
+            biases[b] = bias
+            nc.vector.tensor_tensor(
+                out=bias[:], in0=stat_ps[b][:, :, b], in1=params[:, 0:4], op=ALU.add
+            )
+
+        def relu(b, ht):
+            if ht == 0:
+                u = two.tile([P, H_TILES, T], F32, tag="u")
+                relu_out[b] = u
+            if b == B - 1 and ht % 2 == 0:
+                nc.vector.tensor_scalar(
+                    out=relu_out[b][:, ht, :], in0=main_ps[b][ht][:],
+                    scalar1=biases[b][:, ht : ht + 1], scalar2=0.0, op0=ALU.add, op1=ALU.max,
+                )
+            else:
                 nc.scalar.activation(
-                    out=u[:, ht, :], in_=acc[:], func=ACT.Relu, bias=bias[:, ht : ht + 1], scale=1.0
+                    out=relu_out[b][:, ht, :], in_=main_ps[b][ht][:], func=ACT.Relu,
+                    bias=biases[b][:, ht : ht + 1], scale=1.0,
                 )
 
-        def layer_norm(b):
-            u = relu_out[b]
-            normed = two.tile([P, T_TILES, H], F32, tag="normed")
-            for pair in range(2):
-                ln_stats = four.tile([P, 2, 6], F32, tag="ln_stats")
-                mean_var = four.tile([P, 2, 2], F32, tag="mean_var")
-                banks = []
-                for i in range(2):
-                    tb = 2 * pair + i
-                    u_t = ps_first.tile([P, H], F32, tag="first")
-                    for ht in range(H_TILES):
-                        nc.tensor.transpose(
-                            u_t[:, P * ht : P * (ht + 1)], u[:, ht, P * tb : P * (tb + 1)],
-                            ident_f32[:],
-                        )
-                    nc.vector.bn_stats(out=ln_stats[:, i, :], in_=u_t[:])
-                    nc.vector.bn_aggr(out=mean_var[:, i, :], in_=ln_stats[:, i, :])
-                    banks.append(u_t)
-                var_eps = four.tile([P, 2], F32, tag="var_eps")
-                nc.vector.tensor_scalar_add(out=var_eps[:], in0=mean_var[:, :, 1], scalar1=EPS_LN)
-                neg_mean = four.tile([P, 2], F32, tag="neg_mean")
-                nc.vector.tensor_scalar_mul(out=neg_mean[:], in0=mean_var[:, :, 0], scalar1=-1.0)
-                rstd = four.tile([P, 2], F32, tag="rstd")
-                nc.gpsimd.tensor_tensor(
-                    out=rstd[:], in0=var_eps[:], in1=minus_half[:, 0:2], op=ALU.pow
-                )
-                shift = four.tile([P, 2], F32, tag="shift")
-                nc.gpsimd.tensor_tensor(out=shift[:], in0=neg_mean[:], in1=rstd[:], op=ALU.mult)
-                for i in range(2):
-                    nc.scalar.activation(
-                        out=normed[:, 2 * pair + i, :], in_=banks[i][:], func=ACT.Identity,
-                        scale=rstd[:, i : i + 1], bias=shift[:, i : i + 1],
-                    )
-            for ht in range(H_TILES):
-                back = ps_back.tile([P, T], F32, tag="back")
-                for tb in range(T_TILES):
+        def transpose_u(b, pair):
+            for tb in range(2 * pair, 2 * pair + 2):
+                u_t = ps_first.tile([P, H], F32, tag="first")
+                u_banks[(b, tb)] = u_t
+                for ht in range(H_TILES):
                     nc.tensor.transpose(
-                        back[:, P * tb : P * (tb + 1)], normed[:, tb, P * ht : P * (ht + 1)],
-                        ident_f32[:],
+                        u_t[:, P * ht : P * (ht + 1)],
+                        relu_out[b][:, ht, P * tb : P * (tb + 1)], ident_f32[:],
                     )
-                result = four.tile([P, T], F32, tag="result")
-                nc.scalar.activation(
-                    out=result[:], in_=back[:], func=ACT.Tanh,
-                    scale=params[:, 4 + ht : 5 + ht], bias=params[:, 8 + ht : 9 + ht],
-                )
-                nc.sync.dma_start(out=out[b, P * ht : P * (ht + 1), :], in_=result[:])
 
-        for g in range(X_PASSES):
+        def frame_stats(b, pair):
+            ln_stats = four.tile([P, 2, 6], F32, tag="ln_stats")
+            mean_var = four.tile([P, 2, 2], F32, tag="mean_var")
+            for i in range(2):
+                nc.vector.bn_stats(out=ln_stats[:, i, :], in_=u_banks[(b, 2 * pair + i)][:])
+            for i in range(2):
+                nc.vector.bn_aggr(out=mean_var[:, i, :], in_=ln_stats[:, i, :])
+            var_eps = four.tile([P, 2], F32, tag="var_eps")
+            nc.gpsimd.tensor_scalar(
+                out=var_eps[:], in0=mean_var[:, :, 1], scalar1=1.0, scalar2=EPS_LN,
+                op0=ALU.mult, op1=ALU.add,
+            )
+            rstd = four.tile([P, 2], F32, tag="rstd")
+            nc.gpsimd.tensor_tensor(
+                out=rstd[:], in0=var_eps[:], in1=minus_half[:, 0:2], op=ALU.pow
+            )
+            neg_mean = four.tile([P, 2], F32, tag="neg_mean")
+            nc.gpsimd.tensor_scalar(
+                out=neg_mean[:], in0=mean_var[:, :, 0], scalar1=-1.0, scalar2=0.0,
+                op0=ALU.mult, op1=ALU.add,
+            )
+            shift = four.tile([P, 2], F32, tag="shift")
+            nc.gpsimd.tensor_tensor(out=shift[:], in0=neg_mean[:], in1=rstd[:], op=ALU.mult)
+            scales[(b, pair)] = (rstd, shift)
+
+        def normalise(b, tb):
+            if tb == 0:
+                normed = four.tile([P, T_TILES, H], F32, tag="normed")
+                normed_out[b] = normed
+            pair, i = divmod(tb, 2)
+            rstd, shift = scales[(b, pair)]
+            if b == B - 1 and i == 0:
+                nc.vector.tensor_scalar(
+                    out=normed_out[b][:, tb, :], in0=u_banks[(b, tb)][:],
+                    scalar1=rstd[:, i : i + 1], scalar2=shift[:, i : i + 1],
+                    op0=ALU.mult, op1=ALU.add,
+                )
+            else:
+                nc.scalar.activation(
+                    out=normed_out[b][:, tb, :], in_=u_banks[(b, tb)][:], func=ACT.Identity,
+                    scale=rstd[:, i : i + 1], bias=shift[:, i : i + 1],
+                )
+
+        def finish(b, ht, blocks):
+            frames = slice(P * blocks.start, P * blocks.stop)
+            back = ps_mx.tile([P, T], F32, tag="mx")
+            for tb in blocks:
+                nc.tensor.transpose(
+                    back[:, P * tb : P * (tb + 1)],
+                    normed_out[b][:, tb, P * ht : P * (ht + 1)],
+                    ident_f32[:],
+                )
+            if blocks.start == 0:
+                result = five.tile([P, T], F32, tag="result")
+                results[(b, ht)] = result
+            result = results[(b, ht)]
+            nc.scalar.activation(
+                out=result[:, frames], in_=back[:, frames], func=ACT.Tanh,
+                scale=params[:, 4 + ht : 5 + ht], bias=params[:, 8 + ht : 9 + ht],
+            )
+            nc.sync.dma_start(out=out[b, P * ht : P * (ht + 1), frames], in_=result[:, frames])
+
+        TILES = range(H_TILES)
+        SLOT = range(SLOTS)
+        ALL = range(X_PASSES)
+        last = B - 1
+
+        def first_products(b):
+            main_product(b, range(3))
+
+        def bias_and_relu(b):
+            add_bias(b)
+            for ht in TILES:
+                if ht == 3:
+                    main_product(b, range(3, 4))
+                relu(b, ht)
+
+        spread_mask(0)
+        for g in ALL:
             group_x(0, g)
-            masked_stats(0, g)
-        x_tiles.append(load_x(2))
-        nc.vector.reciprocal(out=inv_sum[:], in_=mask_sum[:])
-        nc.vector.tensor_scalar_mul(out=inv_sum_256[:], in0=inv_sum[:], scalar1=256.0)
-        mean_and_std(0)
+        mask_x(0, 0)
+        mask_x(0, 1)
+        channel_stats(0, 0, SLOT)
+        channel_sums(0, 0, nc.gpsimd)
+        mask_x(0, 2)
+        channel_stats(0, 1, SLOT)
+        channel_sums(0, 1, nc.gpsimd)
+        invert_mask_sum(0)
+        channel_stats(0, 2, SLOT)
+        channel_sums(0, 2, nc.gpsimd)
+        for g in ALL:
+            quantise_x(0, g)
+        mean_and_var(0, ALL, nc.gpsimd)
         for g in range(W_PASSES):
             transpose_w(g)
             quantise_w(g)
-            if g == X_PASSES - 1:
-                x_tiles.append(load_x(3))
-        for g in range(X_PASSES):
-            quantise_x(0, g)
+            if g in (2, 4, 6):
+                spread_mask(g // 2)
+            if g == 4:
+                square_root(0)
         param_ps = ps_mx.tile([P, P], BF16, tag="mx")
         nc.tensor.transpose(param_ps[:], param_rows[:], ident_bf16[:])
         nc.vector.tensor_copy(out=params[:], in_=param_ps[:, 0:12])
+        group_x(1, 0)
+        quantise_stats(0)
+        mask_x(1, 0)
+        mask_x(1, 1)
+        first_products(0)
         stat_product(0)
-        main_product(0)
-        for b in range(1, B):
-            for g in range(X_PASSES):
-                group_x(b, g)
-                masked_stats(b, g)
-                if b == 3 and g == 0:
-                    layer_norm(1)
-            if b == 2:
-                layer_norm(0)
-            mean_and_std(b)
-            for g in range(X_PASSES):
-                quantise_x(b, g)
+        group_x(1, 1)
+        channel_stats(1, 0, range(0, 2))
+        bias_and_relu(0)
+        channel_stats(1, 0, range(2, 4))
+        channel_sums(1, 0, nc.gpsimd)
+        group_x(1, 2)
+        quantise_x(1, 0)
+        for b in range(1, last):
+            mask_x(b, 2)
+            channel_stats(b, 1, range(0, 2))
+            if b > 1:
+                bias_and_relu(b - 1)
+            channel_stats(b, 1, range(2, 4))
+            channel_sums(b, 1, nc.gpsimd)
+            invert_mask_sum(b)
+            quantise_x(b, 1)
+            group_x(b + 1, 0)
+            mask_x(b + 1, 0)
+            for pair in range(2):
+                transpose_u(b - 1, pair)
+            frame_stats(b - 1, 0)
+            group_x(b + 1, 1)
+            channel_stats(b, 2, range(0, 2))
+            frame_stats(b - 1, 1)
+            channel_stats(b, 2, range(2, 4))
+            quantise_x(b, 2)
+            channel_sums(b, 2, nc.gpsimd)
+            mean_and_var(b, ALL, nc.gpsimd)
+            for tb in range(T_TILES):
+                normalise(b - 1, tb)
+            square_root(b)
+            group_x(b + 1, 2)
+            mask_x(b + 1, 1)
+            first_products(b)
+            channel_stats(b + 1, 0, range(0, 3))
+            quantise_stats(b)
             stat_product(b)
-            if b == 3:
-                layer_norm(2)
-            main_product(b)
-        layer_norm(3)
+            channel_stats(b + 1, 0, range(3, 4))
+            channel_sums(b + 1, 0, nc.gpsimd)
+            quantise_x(b + 1, 0)
+        mask_x(last, 2)
+        channel_stats(last, 1, range(0, 2))
+        bias_and_relu(last - 1)
+        for pair in range(2):
+            transpose_u(last - 1, pair)
+        for b in range(last - 1):
+            for ht in TILES:
+                finish(b, ht, range(T_TILES))
+        channel_stats(last, 1, range(2, 4))
+        channel_sums(last, 1, nc.gpsimd)
+        invert_mask_sum(last)
+        quantise_x(last, 1)
+        mean_and_var(last, range(0, 2), nc.gpsimd)
+        power_root(last, range(0, 2))
+        quantise_x(last, 2)
+        first_products(last)
+        channel_stats(last, 2, SLOT)
+        channel_sums(last, 2, nc.vector)
+        mean_and_var(last, range(2, 3), nc.vector)
+        power_root(last, range(2, 3))
+        frame_stats(last - 1, 0)
+        quantise_stats(last)
+        stat_product(last)
+        frame_stats(last - 1, 1)
+        normalise(last - 1, 0)
+        normalise(last - 1, 1)
+        bias_and_relu(last)
+        normalise(last - 1, 2)
+        normalise(last - 1, 3)
+        transpose_u(last, 0)
+        transpose_u(last, 1)
+        frame_stats(last, 0)
+        for ht in TILES:
+            finish(last - 1, ht, range(T_TILES))
+        frame_stats(last, 1)
+        for pair in range(2):
+            for i in range(2):
+                normalise(last, 2 * pair + i)
+            for ht in TILES:
+                finish(last, ht, range(2 * pair, 2 * pair + 2))

@@ -446,36 +446,48 @@ def tile_attentivestatspool_pa_kernel(tc, x, mask, w1, b1, g1, be1, out):
         for g in ALL:
             quantise_x(0, g)
         mean_and_var(0, ALL, nc.gpsimd)
-        for g in range(W_PASSES):
+        spread_mask(1)
+        for g in range(5):
             transpose_w(g)
-            quantise_w(g)
-            if g in (2, 4, 6):
-                spread_mask(g // 2)
-            if g == 4:
-                square_root(0)
-        param_ps = ps_mx.tile([P, P], BF16, tag="mx")
-        nc.tensor.transpose(param_ps[:], param_rows[:], ident_bf16[:])
-        nc.vector.tensor_copy(out=params[:], in_=param_ps[:, 0:12])
-        group_x(1, 0)
-        quantise_stats(0)
         mask_x(1, 0)
         mask_x(1, 1)
+        for g in range(5):
+            quantise_w(g)
+        spread_mask(2)
+        for g in range(5, 7):
+            transpose_w(g)
+        square_root(0)
+        channel_stats(1, 0, SLOT)
+        channel_sums(1, 0, nc.gpsimd)
+        for g in range(5, 7):
+            quantise_w(g)
+        spread_mask(3)
+        for g in range(7, W_PASSES):
+            transpose_w(g)
+        param_ps = ps_mx.tile([P, P], BF16, tag="mx")
+        nc.tensor.transpose(param_ps[:], param_rows[:], ident_bf16[:])
+        group_x(1, 0)
+        mask_x(1, 2)
+        channel_stats(1, 1, range(0, 2))
+        for g in range(7, W_PASSES):
+            quantise_w(g)
+        nc.vector.tensor_copy(out=params[:], in_=param_ps[:, 0:12])
+        quantise_stats(0)
         first_products(0)
         stat_product(0)
         group_x(1, 1)
-        channel_stats(1, 0, range(0, 2))
-        bias_and_relu(0)
-        channel_stats(1, 0, range(2, 4))
-        channel_sums(1, 0, nc.gpsimd)
-        group_x(1, 2)
+        channel_stats(1, 1, range(2, 4))
+        channel_sums(1, 1, nc.gpsimd)
         quantise_x(1, 0)
+        bias_and_relu(0)
+        group_x(1, 2)
         for b in range(1, last):
-            mask_x(b, 2)
-            channel_stats(b, 1, range(0, 2))
             if b > 1:
+                mask_x(b, 2)
+                channel_stats(b, 1, range(0, 2))
                 bias_and_relu(b - 1)
-            channel_stats(b, 1, range(2, 4))
-            channel_sums(b, 1, nc.gpsimd)
+                channel_stats(b, 1, range(2, 4))
+                channel_sums(b, 1, nc.gpsimd)
             invert_mask_sum(b)
             quantise_x(b, 1)
             group_x(b + 1, 0)

@@ -123,12 +123,12 @@ def tile_attentivestatspool_pa_kernel(tc, x, mask, w1, b1, g1, be1, out):
                 )
         inv_sum = const.tile([P, B], F32)
         inv_sum_256 = const.tile([P, B], F32)
+        inv_sum_256_sq = const.tile([P, B], F32)
         params = const.tile([P, 12], F32)
 
         masked = {}
         stats = {}
-        moments = {}
-        sums = {}
+        variances = {}
         x_grouped = {}
         x_quant = {}
         w_grouped = {}
@@ -152,12 +152,16 @@ def tile_attentivestatspool_pa_kernel(tc, x, mask, w1, b1, g1, be1, out):
                 op=ALU.mult,
             )
 
-        def channel_stats(b, g, slots):
-            if (b, g) not in stats:
-                stats_bg = four.tile([P, SLOTS, 6], F32, tag="stats")
-                stats[(b, g)] = stats_bg
-            for j in slots:
-                nc.vector.bn_stats(out=stats[(b, g)][:, j, :], in_=masked[(b, g)][:, j, :])
+        def channel_stats(b, g, slots, between=()):
+            if g == 0 and slots.start == 0:
+                stats_b = two.tile([P, ROWS, 6], F32, tag="stats")
+                stats[b] = stats_b
+            for n, j in enumerate(slots):
+                nc.vector.bn_stats(
+                    out=stats[b][:, SLOTS * g + j, :], in_=masked[(b, g)][:, j, :]
+                )
+                for step in between[2 * n : 2 * n + 2]:
+                    step()
 
         def transpose_w(g):
             third, g_in = divmod(g, X_PASSES)
@@ -209,64 +213,71 @@ def tile_attentivestatspool_pa_kernel(tc, x, mask, w1, b1, g1, be1, out):
                 in_=x_grouped[(b, g)][:].rearrange("p t j -> p (t j)"),
             )
 
-        def channel_sums(b, g, engine):
-            if g == 0:
-                sum_x = two.tile([P, X_PASSES, SLOTS], F32, tag="sum_x")
-                sum_sq = two.tile([P, X_PASSES, SLOTS], F32, tag="sum_sq")
-                sums[b] = (sum_x, sum_sq)
-            sum_x, sum_sq = sums[b]
-            halves = stats[(b, g)][:].rearrange("p j (h s) -> p j h s", s=3)
-            mean_sq = two.tile([P, SLOTS, 2], F32, tag="mean_sq")
-            engine.tensor_tensor(
-                out=mean_sq[:], in0=halves[:, :, :, 1], in1=halves[:, :, :, 1], op=ALU.mult
-            )
-            dev = two.tile([P, SLOTS, 2], F32, tag="dev")
-            engine.tensor_scalar(
-                out=dev[:], in0=halves[:, :, :, 2], scalar1=1.0 / 256.0, scalar2=0.0,
-                op0=ALU.mult, op1=ALU.add,
-            )
-            engine.tensor_tensor(
-                out=sum_x[:, g, :], in0=halves[:, :, 0, 1], in1=halves[:, :, 1, 1], op=ALU.add
-            )
-            half_sq = two.tile([P, SLOTS, 2], F32, tag="half_sq")
-            engine.tensor_tensor(out=half_sq[:], in0=mean_sq[:], in1=dev[:], op=ALU.add)
-            engine.tensor_tensor(
-                out=sum_sq[:, g, :], in0=half_sq[:, :, 0], in1=half_sq[:, :, 1], op=ALU.add
-            )
+        def stat_steps(b, groups):
+            rows = slice(SLOTS * groups.start, SLOTS * groups.stop)
+            n = SLOTS * len(groups)
+            if groups.start == 0:
+                var0 = two.tile([P, ROWS], F32, tag="var0")
+                variances[b] = var0
+            var0 = variances[b]
+            half_mean = stats[b][:, rows, :].rearrange("p r (h s) -> p r h s", s=3)[:, :, :, 1]
+            half_dev = stats[b][:, rows, :].rearrange("p r (h s) -> p r h s", s=3)[:, :, :, 2]
+            mean_sq = two.tile([P, ROWS, 2], F32, tag="mean_sq")
+            half_sq = two.tile([P, ROWS, 2], F32, tag="half_sq")
+            sum_mean = two.tile([P, ROWS], F32, tag="sum_mean")
+            sum_sq = two.tile([P, ROWS], F32, tag="sum_sq")
+            mean0_sq = two.tile([P, ROWS], F32, tag="mean0_sq")
+            diff = two.tile([P, ROWS], F32, tag="diff")
+            return [
+                lambda: nc.vector.tensor_tensor(
+                    out=mean_sq[:, 0:n, :], in0=half_mean, in1=half_mean, op=ALU.mult
+                ),
+                lambda: nc.vector.tensor_tensor(
+                    out=sum_mean[:, 0:n], in0=half_mean[:, :, 0], in1=half_mean[:, :, 1],
+                    op=ALU.add,
+                ),
+                lambda: nc.vector.scalar_tensor_tensor(
+                    out=half_sq[:, 0:n, :], in0=mean_sq[:, 0:n, :], scalar=256.0, in1=half_dev,
+                    op0=ALU.mult, op1=ALU.add,
+                ),
+                lambda: nc.vector.scalar_tensor_tensor(
+                    out=mean0_sq[:, 0:n], in0=sum_mean[:, 0:n],
+                    scalar=inv_sum_256_sq[:, b : b + 1], in1=sum_mean[:, 0:n],
+                    op0=ALU.mult, op1=ALU.mult,
+                ),
+                lambda: nc.vector.tensor_tensor(
+                    out=sum_sq[:, 0:n], in0=half_sq[:, 0:n, 0], in1=half_sq[:, 0:n, 1],
+                    op=ALU.add,
+                ),
+                lambda: nc.vector.tensor_scalar_mul(
+                    out=stat_in[:, groups.start : groups.stop, b, :],
+                    in0=sum_mean[:, 0:n].rearrange("p (g j) -> p g j", j=SLOTS),
+                    scalar1=inv_sum_256[:, b : b + 1],
+                ),
+                lambda: nc.vector.scalar_tensor_tensor(
+                    out=diff[:, 0:n], in0=sum_sq[:, 0:n], scalar=inv_sum[:, b : b + 1],
+                    in1=mean0_sq[:, 0:n], op0=ALU.mult, op1=ALU.subtract,
+                ),
+                lambda: nc.vector.tensor_scalar_max(
+                    out=var0[:, rows], in0=diff[:, 0:n], scalar1=EPS_STD
+                ),
+            ]
 
         def invert_mask_sum(b):
             nc.vector.reciprocal(out=inv_sum[:, b : b + 1], in_=mask_sum[:, b : b + 1])
             nc.vector.tensor_scalar_mul(
                 out=inv_sum_256[:, b : b + 1], in0=inv_sum[:, b : b + 1], scalar1=256.0
             )
-
-        def mean_and_var(b, groups, engine):
-            if groups.start == 0:
-                mean0 = two.tile([P, X_PASSES, SLOTS], F32, tag="mean0")
-                var0 = two.tile([P, X_PASSES, SLOTS], F32, tag="var0")
-                moments[b] = (mean0, var0)
-            mean0, var0 = moments[b]
-            gs = slice(groups.start, groups.stop)
-            sum_x, sum_sq = sums[b]
-            scale = inv_sum_256[:, b : b + 1]
-            engine.tensor_scalar_mul(out=mean0[:, gs, :], in0=sum_x[:, gs, :], scalar1=scale)
-            mean0_sq = two.tile([P, X_PASSES, SLOTS], F32, tag="mean0_sq")
-            engine.tensor_tensor(
-                out=mean0_sq[:, gs, :], in0=mean0[:, gs, :], in1=mean0[:, gs, :], op=ALU.mult
+            nc.vector.tensor_tensor(
+                out=inv_sum_256_sq[:, b : b + 1], in0=inv_sum_256[:, b : b + 1],
+                in1=inv_sum_256[:, b : b + 1], op=ALU.mult,
             )
-            mean_sq0 = two.tile([P, X_PASSES, SLOTS], F32, tag="mean_sq0")
-            engine.tensor_scalar_mul(out=mean_sq0[:, gs, :], in0=sum_sq[:, gs, :], scalar1=scale)
-            diff = two.tile([P, X_PASSES, SLOTS], F32, tag="diff")
-            engine.tensor_tensor(
-                out=diff[:, gs, :], in0=mean_sq0[:, gs, :], in1=mean0_sq[:, gs, :],
-                op=ALU.subtract,
-            )
-            engine.tensor_scalar_max(out=var0[:, gs, :], in0=diff[:, gs, :], scalar1=EPS_STD)
-            engine.tensor_copy(out=stat_in[:, gs, b, :], in_=mean0[:, gs, :])
 
         def square_root(b):
             nc.scalar.activation(
-                out=stat_in[:, X_PASSES : 2 * X_PASSES, b, :], in_=moments[b][1][:], func=ACT.Sqrt
+                out=stat_in[:, X_PASSES : 2 * X_PASSES, b, :], in_=variances[b][:].rearrange(
+                    "p (g j) -> p g j", j=SLOTS
+                ), func=ACT.Sqrt
             )
 
         def power_root(b, groups):
@@ -274,7 +285,8 @@ def tile_attentivestatspool_pa_kernel(tc, x, mask, w1, b1, g1, be1, out):
             n = len(groups)
             nc.gpsimd.tensor_tensor(
                 out=stat_in[:, X_PASSES + groups.start : X_PASSES + groups.stop, b, :],
-                in0=moments[b][1][:, gs, :], in1=half[:, 0:n, :], op=ALU.pow,
+                in0=variances[b][:].rearrange("p (g j) -> p g j", j=SLOTS)[:, gs, :],
+                in1=half[:, 0:n, :], op=ALU.pow,
             )
 
         def quantise_stats(b):
@@ -353,47 +365,50 @@ def tile_attentivestatspool_pa_kernel(tc, x, mask, w1, b1, g1, be1, out):
                         relu_out[b][:, ht, P * tb : P * (tb + 1)], ident_f32[:],
                     )
 
-        def frame_stats(b, pair):
-            ln_stats = four.tile([P, 2, 6], F32, tag="ln_stats")
-            mean_var = four.tile([P, 2, 2], F32, tag="mean_var")
-            for i in range(2):
-                nc.vector.bn_stats(out=ln_stats[:, i, :], in_=u_banks[(b, 2 * pair + i)][:])
-            for i in range(2):
+        def frame_stats(b, blocks):
+            n = len(blocks)
+            ln_stats = four.tile([P, T_TILES, 6], F32, tag="ln_stats")
+            mean_var = four.tile([P, T_TILES, 2], F32, tag="mean_var")
+            for i, tb in enumerate(blocks):
+                nc.vector.bn_stats(out=ln_stats[:, i, :], in_=u_banks[(b, tb)][:])
+            for i in range(n):
                 nc.vector.bn_aggr(out=mean_var[:, i, :], in_=ln_stats[:, i, :])
-            var_eps = four.tile([P, 2], F32, tag="var_eps")
+            var_eps = four.tile([P, T_TILES], F32, tag="var_eps")
             nc.gpsimd.tensor_scalar(
-                out=var_eps[:], in0=mean_var[:, :, 1], scalar1=1.0, scalar2=EPS_LN,
+                out=var_eps[:, 0:n], in0=mean_var[:, 0:n, 1], scalar1=1.0, scalar2=EPS_LN,
                 op0=ALU.mult, op1=ALU.add,
             )
-            rstd = four.tile([P, 2], F32, tag="rstd")
+            rstd = four.tile([P, T_TILES], F32, tag="rstd")
             nc.gpsimd.tensor_tensor(
-                out=rstd[:], in0=var_eps[:], in1=minus_half[:, 0:2], op=ALU.pow
+                out=rstd[:, 0:n], in0=var_eps[:, 0:n], in1=minus_half[:, 0:n], op=ALU.pow
             )
-            neg_mean = four.tile([P, 2], F32, tag="neg_mean")
+            neg_mean = four.tile([P, T_TILES], F32, tag="neg_mean")
             nc.gpsimd.tensor_scalar(
-                out=neg_mean[:], in0=mean_var[:, :, 0], scalar1=-1.0, scalar2=0.0,
+                out=neg_mean[:, 0:n], in0=mean_var[:, 0:n, 0], scalar1=-1.0, scalar2=0.0,
                 op0=ALU.mult, op1=ALU.add,
             )
-            shift = four.tile([P, 2], F32, tag="shift")
-            nc.gpsimd.tensor_tensor(out=shift[:], in0=neg_mean[:], in1=rstd[:], op=ALU.mult)
-            scales[(b, pair)] = (rstd, shift)
+            shift = four.tile([P, T_TILES], F32, tag="shift")
+            nc.gpsimd.tensor_tensor(
+                out=shift[:, 0:n], in0=neg_mean[:, 0:n], in1=rstd[:, 0:n], op=ALU.mult
+            )
+            for i, tb in enumerate(blocks):
+                scales[(b, tb)] = (rstd[:, i : i + 1], shift[:, i : i + 1])
 
         def normalise(b, tb):
             if tb == 0:
                 normed = four.tile([P, T_TILES, H], F32, tag="normed")
                 normed_out[b] = normed
-            pair, i = divmod(tb, 2)
-            rstd, shift = scales[(b, pair)]
-            if b == B - 1 and i == 0:
+            rstd, shift = scales[(b, tb)]
+            if b == B - 1 and tb % 2 == 0:
                 nc.vector.tensor_scalar(
                     out=normed_out[b][:, tb, :], in0=u_banks[(b, tb)][:],
-                    scalar1=rstd[:, i : i + 1], scalar2=shift[:, i : i + 1],
+                    scalar1=rstd, scalar2=shift,
                     op0=ALU.mult, op1=ALU.add,
                 )
             else:
                 nc.scalar.activation(
                     out=normed_out[b][:, tb, :], in_=u_banks[(b, tb)][:], func=ACT.Identity,
-                    scale=rstd[:, i : i + 1], bias=shift[:, i : i + 1],
+                    scale=rstd, bias=shift,
                 )
 
         def finish(b, ht, blocks):
@@ -436,21 +451,22 @@ def tile_attentivestatspool_pa_kernel(tc, x, mask, w1, b1, g1, be1, out):
         mask_x(0, 0)
         mask_x(0, 1)
         channel_stats(0, 0, SLOT)
-        channel_sums(0, 0, nc.gpsimd)
         mask_x(0, 2)
         channel_stats(0, 1, SLOT)
-        channel_sums(0, 1, nc.gpsimd)
         invert_mask_sum(0)
         channel_stats(0, 2, SLOT)
-        channel_sums(0, 2, nc.gpsimd)
+        steps = stat_steps(0, ALL)
         for g in ALL:
             quantise_x(0, g)
-        mean_and_var(0, ALL, nc.gpsimd)
+            for step in steps[2 * g : 2 * g + 2]:
+                step()
         spread_mask(1)
+        mask_x(1, 0)
+        for step in steps[6:]:
+            step()
+        mask_x(1, 1)
         for g in range(5):
             transpose_w(g)
-        mask_x(1, 0)
-        mask_x(1, 1)
         for g in range(5):
             quantise_w(g)
         spread_mask(2)
@@ -458,7 +474,6 @@ def tile_attentivestatspool_pa_kernel(tc, x, mask, w1, b1, g1, be1, out):
             transpose_w(g)
         square_root(0)
         channel_stats(1, 0, SLOT)
-        channel_sums(1, 0, nc.gpsimd)
         for g in range(5, 7):
             quantise_w(g)
         spread_mask(3)
@@ -477,7 +492,6 @@ def tile_attentivestatspool_pa_kernel(tc, x, mask, w1, b1, g1, be1, out):
         stat_product(0)
         group_x(1, 1)
         channel_stats(1, 1, range(2, 4))
-        channel_sums(1, 1, nc.gpsimd)
         quantise_x(1, 0)
         bias_and_relu(0)
         group_x(1, 2)
@@ -487,33 +501,27 @@ def tile_attentivestatspool_pa_kernel(tc, x, mask, w1, b1, g1, be1, out):
                 channel_stats(b, 1, range(0, 2))
                 bias_and_relu(b - 1)
                 channel_stats(b, 1, range(2, 4))
-                channel_sums(b, 1, nc.gpsimd)
             invert_mask_sum(b)
             quantise_x(b, 1)
             group_x(b + 1, 0)
             mask_x(b + 1, 0)
             for pair in range(2):
                 transpose_u(b - 1, pair)
-            frame_stats(b - 1, 0)
             group_x(b + 1, 1)
             channel_stats(b, 2, range(0, 2))
-            frame_stats(b - 1, 1)
+            frame_stats(b - 1, range(T_TILES))
             channel_stats(b, 2, range(2, 4))
             quantise_x(b, 2)
-            channel_sums(b, 2, nc.gpsimd)
-            mean_and_var(b, ALL, nc.gpsimd)
             for tb in range(T_TILES):
                 normalise(b - 1, tb)
-            square_root(b)
             group_x(b + 1, 2)
             mask_x(b + 1, 1)
             first_products(b)
-            channel_stats(b + 1, 0, range(0, 3))
+            channel_stats(b + 1, 0, SLOT, stat_steps(b, ALL))
+            square_root(b)
+            quantise_x(b + 1, 0)
             quantise_stats(b)
             stat_product(b)
-            channel_stats(b + 1, 0, range(3, 4))
-            channel_sums(b + 1, 0, nc.gpsimd)
-            quantise_x(b + 1, 0)
         mask_x(last, 2)
         channel_stats(last, 1, range(0, 2))
         bias_and_relu(last - 1)
@@ -523,21 +531,19 @@ def tile_attentivestatspool_pa_kernel(tc, x, mask, w1, b1, g1, be1, out):
             for ht in TILES:
                 finish(b, ht, range(T_TILES))
         channel_stats(last, 1, range(2, 4))
-        channel_sums(last, 1, nc.gpsimd)
         invert_mask_sum(last)
         quantise_x(last, 1)
-        mean_and_var(last, range(0, 2), nc.gpsimd)
-        power_root(last, range(0, 2))
         quantise_x(last, 2)
         first_products(last)
-        channel_stats(last, 2, SLOT)
-        channel_sums(last, 2, nc.vector)
-        mean_and_var(last, range(2, 3), nc.vector)
+        channel_stats(last, 2, SLOT, stat_steps(last, range(0, 2)))
+        power_root(last, range(0, 2))
+        for step in stat_steps(last, range(2, 3)):
+            step()
         power_root(last, range(2, 3))
-        frame_stats(last - 1, 0)
+        frame_stats(last - 1, range(0, 2))
         quantise_stats(last)
         stat_product(last)
-        frame_stats(last - 1, 1)
+        frame_stats(last - 1, range(2, 4))
         normalise(last - 1, 0)
         normalise(last - 1, 1)
         bias_and_relu(last)
@@ -545,10 +551,10 @@ def tile_attentivestatspool_pa_kernel(tc, x, mask, w1, b1, g1, be1, out):
         normalise(last - 1, 3)
         transpose_u(last, 0)
         transpose_u(last, 1)
-        frame_stats(last, 0)
+        frame_stats(last, range(0, 2))
         for ht in TILES:
             finish(last - 1, ht, range(T_TILES))
-        frame_stats(last, 1)
+        frame_stats(last, range(2, 4))
         for pair in range(2):
             for i in range(2):
                 normalise(last, 2 * pair + i)

@@ -99,6 +99,9 @@ def tile_attentivestatspool_pa_kernel(tc, x, mask, w1, b1, g1, be1, out):
         nc.gpsimd.memset(stat_in[:].rearrange("p s n j -> p (s n j)").bitcast(F32), 0.0)
         half = const.tile([P, X_PASSES, SLOTS], F32)
         nc.gpsimd.memset(half[:], 0.5)
+        eps_ln = const.tile([P, 1], F32)
+        nc.vector.memset(eps_ln[:], 0.0)
+        nc.vector.tensor_scalar_add(out=eps_ln[:], in0=eps_ln[:], scalar1=EPS_LN)
         minus_half = const.tile([P, 4], F32)
         nc.gpsimd.memset(minus_half[:], -0.5)
 
@@ -139,6 +142,8 @@ def tile_attentivestatspool_pa_kernel(tc, x, mask, w1, b1, g1, be1, out):
         biases = {}
         relu_out = {}
         u_banks = {}
+        frame_moments = {}
+        deviations = {}
         scales = {}
         normed_out = {}
 
@@ -162,6 +167,8 @@ def tile_attentivestatspool_pa_kernel(tc, x, mask, w1, b1, g1, be1, out):
                 )
                 for step in between[2 * n : 2 * n + 2]:
                     step()
+            for step in between[2 * len(slots) :]:
+                step()
 
         def transpose_w(g):
             third, g_in = divmod(g, X_PASSES)
@@ -366,13 +373,37 @@ def tile_attentivestatspool_pa_kernel(tc, x, mask, w1, b1, g1, be1, out):
                     )
 
         def frame_stats(b, blocks):
-            n = len(blocks)
             ln_stats = four.tile([P, T_TILES, 6], F32, tag="ln_stats")
             mean_var = four.tile([P, T_TILES, 2], F32, tag="mean_var")
+            frame_moments[(b, blocks.start)] = mean_var
             for i, tb in enumerate(blocks):
                 nc.vector.bn_stats(out=ln_stats[:, i, :], in_=u_banks[(b, tb)][:])
-            for i in range(n):
+            for i in range(len(blocks)):
                 nc.vector.bn_aggr(out=mean_var[:, i, :], in_=ln_stats[:, i, :])
+
+        def frame_deviation(b, blocks):
+            deviation = four.tile([P, T_TILES], F32, tag="deviation")
+            deviations[b] = deviation
+            nc.scalar.activation(
+                out=deviation[:], in_=frame_moments[(b, blocks.start)][:, :, 1], func=ACT.Sqrt,
+                bias=eps_ln[:],
+            )
+
+        def frame_scales(b, blocks):
+            mean_var = frame_moments[(b, blocks.start)]
+            rstd = four.tile([P, T_TILES], F32, tag="rstd")
+            nc.vector.reciprocal(out=rstd[:], in_=deviations[b][:])
+            shift = four.tile([P, T_TILES], F32, tag="shift")
+            nc.vector.scalar_tensor_tensor(
+                out=shift[:], in0=mean_var[:, :, 0], scalar=-1.0, in1=rstd[:],
+                op0=ALU.mult, op1=ALU.mult,
+            )
+            for i, tb in enumerate(blocks):
+                scales[(b, tb)] = (rstd[:, i : i + 1], shift[:, i : i + 1])
+
+        def frame_scales_pow(b, blocks):
+            n = len(blocks)
+            mean_var = frame_moments[(b, blocks.start)]
             var_eps = four.tile([P, T_TILES], F32, tag="var_eps")
             nc.gpsimd.tensor_scalar(
                 out=var_eps[:, 0:n], in0=mean_var[:, 0:n, 1], scalar1=1.0, scalar2=EPS_LN,
@@ -492,58 +523,70 @@ def tile_attentivestatspool_pa_kernel(tc, x, mask, w1, b1, g1, be1, out):
         stat_product(0)
         group_x(1, 1)
         channel_stats(1, 1, range(2, 4))
+        invert_mask_sum(1)
         quantise_x(1, 0)
+        mask_x(2, 0)
         bias_and_relu(0)
         group_x(1, 2)
         for b in range(1, last):
             if b > 1:
                 mask_x(b, 2)
                 channel_stats(b, 1, range(0, 2))
-                bias_and_relu(b - 1)
+                quantise_stats(b - 1)
+                first_products(b - 1)
+                stat_product(b - 1)
                 channel_stats(b, 1, range(2, 4))
-            invert_mask_sum(b)
+                invert_mask_sum(b)
+                mask_x(b + 1, 0)
+                channel_stats(b, 2, range(0, 1))
+                bias_and_relu(b - 1)
             quantise_x(b, 1)
-            group_x(b + 1, 0)
-            mask_x(b + 1, 0)
             for pair in range(2):
                 transpose_u(b - 1, pair)
+            group_x(b + 1, 0)
+            channel_stats(b, 2, range(b - 1, 4))
+            mask_x(b + 1, 1)
             group_x(b + 1, 1)
-            channel_stats(b, 2, range(0, 2))
-            frame_stats(b - 1, range(T_TILES))
-            channel_stats(b, 2, range(2, 4))
             quantise_x(b, 2)
+            frame_stats(b - 1, range(T_TILES))
+            frame_deviation(b - 1, range(T_TILES))
+            channel_stats(b + 1, 0, SLOT, stat_steps(b, ALL))
+            frame_scales(b - 1, range(T_TILES))
             for tb in range(T_TILES):
                 normalise(b - 1, tb)
-            group_x(b + 1, 2)
-            mask_x(b + 1, 1)
-            first_products(b)
-            channel_stats(b + 1, 0, SLOT, stat_steps(b, ALL))
             square_root(b)
+            group_x(b + 1, 2)
             quantise_x(b + 1, 0)
-            quantise_stats(b)
-            stat_product(b)
         mask_x(last, 2)
         channel_stats(last, 1, range(0, 2))
-        bias_and_relu(last - 1)
-        for pair in range(2):
-            transpose_u(last - 1, pair)
-        for b in range(last - 1):
-            for ht in TILES:
-                finish(b, ht, range(T_TILES))
+        for ht in range(3):
+            finish(0, ht, range(T_TILES))
+        quantise_stats(last - 1)
+        stat_product(last - 1)
+        finish(0, 3, range(T_TILES))
+        first_products(last - 1)
         channel_stats(last, 1, range(2, 4))
         invert_mask_sum(last)
         quantise_x(last, 1)
-        quantise_x(last, 2)
-        first_products(last)
-        channel_stats(last, 2, SLOT, stat_steps(last, range(0, 2)))
+        channel_stats(last, 2, range(0, 1))
+        bias_and_relu(last - 1)
+        for pair in range(2):
+            transpose_u(last - 1, pair)
+        for ht in TILES:
+            finish(1, ht, range(T_TILES))
+        channel_stats(last, 2, range(1, 4), stat_steps(last, range(0, 2)))
         power_root(last, range(0, 2))
         for step in stat_steps(last, range(2, 3)):
             step()
         power_root(last, range(2, 3))
+        quantise_x(last, 2)
         frame_stats(last - 1, range(0, 2))
+        frame_scales_pow(last - 1, range(0, 2))
         quantise_stats(last)
+        first_products(last)
         stat_product(last)
         frame_stats(last - 1, range(2, 4))
+        frame_scales_pow(last - 1, range(2, 4))
         normalise(last - 1, 0)
         normalise(last - 1, 1)
         bias_and_relu(last)
@@ -552,9 +595,11 @@ def tile_attentivestatspool_pa_kernel(tc, x, mask, w1, b1, g1, be1, out):
         transpose_u(last, 0)
         transpose_u(last, 1)
         frame_stats(last, range(0, 2))
+        frame_scales_pow(last, range(0, 2))
         for ht in TILES:
             finish(last - 1, ht, range(T_TILES))
         frame_stats(last, range(2, 4))
+        frame_scales_pow(last, range(2, 4))
         for pair in range(2):
             for i in range(2):
                 normalise(last, 2 * pair + i)

@@ -143,6 +143,7 @@ def tile_attentivestatspool_pa_kernel(tc, x, mask, w1, b1, g1, be1, out):
         relu_out = {}
         u_banks = {}
         frame_moments = {}
+        roots = {}
         deviations = {}
         scales = {}
         normed_out = {}
@@ -287,6 +288,9 @@ def tile_attentivestatspool_pa_kernel(tc, x, mask, w1, b1, g1, be1, out):
                 ), func=ACT.Sqrt
             )
 
+        def load_tanh():
+            nc.scalar.activation(out=warm[:], in_=warm[:], func=ACT.Tanh)
+
         def power_root(b, groups):
             gs = slice(groups.start, groups.stop)
             n = len(groups)
@@ -401,26 +405,27 @@ def tile_attentivestatspool_pa_kernel(tc, x, mask, w1, b1, g1, be1, out):
             for i, tb in enumerate(blocks):
                 scales[(b, tb)] = (rstd[:, i : i + 1], shift[:, i : i + 1])
 
-        def frame_scales_pow(b, blocks):
+        def frame_root_pow(b, blocks):
             n = len(blocks)
             mean_var = frame_moments[(b, blocks.start)]
             var_eps = four.tile([P, T_TILES], F32, tag="var_eps")
-            nc.gpsimd.tensor_scalar(
-                out=var_eps[:, 0:n], in0=mean_var[:, 0:n, 1], scalar1=1.0, scalar2=EPS_LN,
-                op0=ALU.mult, op1=ALU.add,
+            nc.vector.tensor_scalar_add(
+                out=var_eps[:, 0:n], in0=mean_var[:, 0:n, 1], scalar1=EPS_LN
             )
             rstd = four.tile([P, T_TILES], F32, tag="rstd")
+            roots[(b, blocks.start)] = rstd
             nc.gpsimd.tensor_tensor(
                 out=rstd[:, 0:n], in0=var_eps[:, 0:n], in1=minus_half[:, 0:n], op=ALU.pow
             )
-            neg_mean = four.tile([P, T_TILES], F32, tag="neg_mean")
-            nc.gpsimd.tensor_scalar(
-                out=neg_mean[:, 0:n], in0=mean_var[:, 0:n, 0], scalar1=-1.0, scalar2=0.0,
-                op0=ALU.mult, op1=ALU.add,
-            )
+
+        def frame_shift(b, blocks):
+            n = len(blocks)
+            mean_var = frame_moments[(b, blocks.start)]
+            rstd = roots[(b, blocks.start)]
             shift = four.tile([P, T_TILES], F32, tag="shift")
-            nc.gpsimd.tensor_tensor(
-                out=shift[:, 0:n], in0=neg_mean[:, 0:n], in1=rstd[:, 0:n], op=ALU.mult
+            nc.vector.scalar_tensor_tensor(
+                out=shift[:, 0:n], in0=mean_var[:, 0:n, 0], scalar=-1.0, in1=rstd[:, 0:n],
+                op0=ALU.mult, op1=ALU.mult,
             )
             for i, tb in enumerate(blocks):
                 scales[(b, tb)] = (rstd[:, i : i + 1], shift[:, i : i + 1])
@@ -430,7 +435,7 @@ def tile_attentivestatspool_pa_kernel(tc, x, mask, w1, b1, g1, be1, out):
                 normed = four.tile([P, T_TILES, H], F32, tag="normed")
                 normed_out[b] = normed
             rstd, shift = scales[(b, tb)]
-            if b == B - 1 and tb % 2 == 0:
+            if b >= B - 2 and tb % 2 == 0:
                 nc.vector.tensor_scalar(
                     out=normed_out[b][:, tb, :], in0=u_banks[(b, tb)][:],
                     scalar1=rstd, scalar2=shift,
@@ -508,6 +513,7 @@ def tile_attentivestatspool_pa_kernel(tc, x, mask, w1, b1, g1, be1, out):
         for g in range(5, 7):
             quantise_w(g)
         spread_mask(3)
+        first_products(0)
         for g in range(7, W_PASSES):
             transpose_w(g)
         param_ps = ps_mx.tile([P, P], BF16, tag="mx")
@@ -519,7 +525,6 @@ def tile_attentivestatspool_pa_kernel(tc, x, mask, w1, b1, g1, be1, out):
             quantise_w(g)
         nc.vector.tensor_copy(out=params[:], in_=param_ps[:, 0:12])
         quantise_stats(0)
-        first_products(0)
         stat_product(0)
         group_x(1, 1)
         channel_stats(1, 1, range(2, 4))
@@ -557,50 +562,56 @@ def tile_attentivestatspool_pa_kernel(tc, x, mask, w1, b1, g1, be1, out):
             square_root(b)
             group_x(b + 1, 2)
             quantise_x(b + 1, 0)
+        load_tanh()
         mask_x(last, 2)
         channel_stats(last, 1, range(0, 2))
-        for ht in range(3):
-            finish(0, ht, range(T_TILES))
         quantise_stats(last - 1)
-        stat_product(last - 1)
-        finish(0, 3, range(T_TILES))
         first_products(last - 1)
+        stat_product(last - 1)
         channel_stats(last, 1, range(2, 4))
         invert_mask_sum(last)
         quantise_x(last, 1)
-        channel_stats(last, 2, range(0, 1))
+        quantise_x(last, 2)
+        steps = stat_steps(last, range(0, 2))
+        channel_stats(last, 2, range(0, 1), steps[0:2])
         bias_and_relu(last - 1)
         for pair in range(2):
             transpose_u(last - 1, pair)
-        for ht in TILES:
-            finish(1, ht, range(T_TILES))
-        channel_stats(last, 2, range(1, 4), stat_steps(last, range(0, 2)))
+        channel_stats(last, 2, range(1, 3), steps[2:8])
         power_root(last, range(0, 2))
+        channel_stats(last, 2, range(3, 4))
         for step in stat_steps(last, range(2, 3)):
             step()
         power_root(last, range(2, 3))
-        quantise_x(last, 2)
+        for ht in TILES:
+            finish(0, ht, range(T_TILES))
+        main_product(last, range(0, 2))
         frame_stats(last - 1, range(0, 2))
-        frame_scales_pow(last - 1, range(0, 2))
+        frame_root_pow(last - 1, range(0, 2))
         quantise_stats(last)
-        first_products(last)
         stat_product(last)
-        frame_stats(last - 1, range(2, 4))
-        frame_scales_pow(last - 1, range(2, 4))
+        main_product(last, range(2, 3))
+        frame_shift(last - 1, range(0, 2))
         normalise(last - 1, 0)
         normalise(last - 1, 1)
+        frame_stats(last - 1, range(2, 4))
+        frame_root_pow(last - 1, range(2, 4))
         bias_and_relu(last)
+        frame_shift(last - 1, range(2, 4))
         normalise(last - 1, 2)
         normalise(last - 1, 3)
         transpose_u(last, 0)
         transpose_u(last, 1)
+        for ht in TILES:
+            finish(1, ht, range(T_TILES))
         frame_stats(last, range(0, 2))
-        frame_scales_pow(last, range(0, 2))
+        frame_root_pow(last, range(0, 2))
+        frame_stats(last, range(2, 4))
+        frame_root_pow(last, range(2, 4))
         for ht in TILES:
             finish(last - 1, ht, range(T_TILES))
-        frame_stats(last, range(2, 4))
-        frame_scales_pow(last, range(2, 4))
         for pair in range(2):
+            frame_shift(last, range(2 * pair, 2 * pair + 2))
             for i in range(2):
                 normalise(last, 2 * pair + i)
             for ht in TILES:

@@ -21,6 +21,7 @@ W_PASSES = 3 * X_PASSES
 ROWS = X_PASSES * SLOTS
 H_TILES = H // P
 T_TILES = T // P
+SCALAR_ROWS = 2
 STAT_STEP = 64
 EPS_LN = 1e-5
 EPS_STD = 1e-5
@@ -131,6 +132,7 @@ def tile_attentivestatspool_pa_kernel(tc, x, mask, w1, b1, g1, be1, out):
 
         masked = {}
         stats = {}
+        sums = {}
         variances = {}
         x_grouped = {}
         x_quant = {}
@@ -221,64 +223,87 @@ def tile_attentivestatspool_pa_kernel(tc, x, mask, w1, b1, g1, be1, out):
                 in_=x_grouped[(b, g)][:].rearrange("p t j -> p (t j)"),
             )
 
+        def new_sums(b):
+            sum_x = two.tile([P, ROWS], F32, tag="sum_x")
+            sum_sq = two.tile([P, ROWS], F32, tag="sum_sq")
+            sums[b] = (sum_x, sum_sq)
+
+        def scalar_sums(b):
+            new_sums(b)
+            sum_x, sum_sq = sums[b]
+            for row in range(ROWS - SCALAR_ROWS, ROWS):
+                channel = masked[(b, X_PASSES - 1)][:, row % SLOTS, :]
+                unused = two.tile([P, T], BF16, tag="unused")
+                nc.scalar.activation(
+                    out=unused[:], in_=channel, func=ACT.Identity, scale=1.0 / 256.0,
+                    accum_out=sum_x[:, row : row + 1],
+                )
+                unused = two.tile([P, T], BF16, tag="unused")
+                nc.scalar.activation(
+                    out=unused[:], in_=channel, func=ACT.Square,
+                    accum_out=sum_sq[:, row : row + 1],
+                )
+
         def stat_steps(b, groups):
             rows = slice(SLOTS * groups.start, SLOTS * groups.stop)
-            n = SLOTS * len(groups)
             if groups.start == 0:
                 var0 = two.tile([P, ROWS], F32, tag="var0")
                 variances[b] = var0
+            if b not in sums:
+                new_sums(b)
             var0 = variances[b]
-            half_mean = stats[b][:, rows, :].rearrange("p r (h s) -> p r h s", s=3)[:, :, :, 1]
-            half_dev = stats[b][:, rows, :].rearrange("p r (h s) -> p r h s", s=3)[:, :, :, 2]
+            sum_x, sum_sq = sums[b]
+            seen = slice(rows.start, min(rows.stop, ROWS - SCALAR_ROWS))
+            half_mean = stats[b][:, seen, :].rearrange("p r (h s) -> p r h s", s=3)[:, :, :, 1]
+            half_dev = stats[b][:, seen, :].rearrange("p r (h s) -> p r h s", s=3)[:, :, :, 2]
             mean_sq = two.tile([P, ROWS, 2], F32, tag="mean_sq")
             half_sq = two.tile([P, ROWS, 2], F32, tag="half_sq")
-            sum_mean = two.tile([P, ROWS], F32, tag="sum_mean")
-            sum_sq = two.tile([P, ROWS], F32, tag="sum_sq")
             mean0_sq = two.tile([P, ROWS], F32, tag="mean0_sq")
             diff = two.tile([P, ROWS], F32, tag="diff")
             return [
                 lambda: nc.vector.tensor_tensor(
-                    out=mean_sq[:, 0:n, :], in0=half_mean, in1=half_mean, op=ALU.mult
+                    out=mean_sq[:, seen, :], in0=half_mean, in1=half_mean, op=ALU.mult
                 ),
                 lambda: nc.vector.tensor_tensor(
-                    out=sum_mean[:, 0:n], in0=half_mean[:, :, 0], in1=half_mean[:, :, 1],
+                    out=sum_x[:, seen], in0=half_mean[:, :, 0], in1=half_mean[:, :, 1],
                     op=ALU.add,
                 ),
                 lambda: nc.vector.scalar_tensor_tensor(
-                    out=half_sq[:, 0:n, :], in0=mean_sq[:, 0:n, :], scalar=256.0, in1=half_dev,
+                    out=half_sq[:, seen, :], in0=mean_sq[:, seen, :], scalar=256.0, in1=half_dev,
                     op0=ALU.mult, op1=ALU.add,
                 ),
                 lambda: nc.vector.scalar_tensor_tensor(
-                    out=mean0_sq[:, 0:n], in0=sum_mean[:, 0:n],
-                    scalar=inv_sum_256_sq[:, b : b + 1], in1=sum_mean[:, 0:n],
+                    out=mean0_sq[:, rows], in0=sum_x[:, rows],
+                    scalar=inv_sum_256_sq[:, b : b + 1], in1=sum_x[:, rows],
                     op0=ALU.mult, op1=ALU.mult,
                 ),
                 lambda: nc.vector.tensor_tensor(
-                    out=sum_sq[:, 0:n], in0=half_sq[:, 0:n, 0], in1=half_sq[:, 0:n, 1],
+                    out=sum_sq[:, seen], in0=half_sq[:, seen, 0], in1=half_sq[:, seen, 1],
                     op=ALU.add,
                 ),
                 lambda: nc.vector.tensor_scalar_mul(
                     out=stat_in[:, groups.start : groups.stop, b, :],
-                    in0=sum_mean[:, 0:n].rearrange("p (g j) -> p g j", j=SLOTS),
+                    in0=sum_x[:, rows].rearrange("p (g j) -> p g j", j=SLOTS),
                     scalar1=inv_sum_256[:, b : b + 1],
                 ),
                 lambda: nc.vector.scalar_tensor_tensor(
-                    out=diff[:, 0:n], in0=sum_sq[:, 0:n], scalar=inv_sum[:, b : b + 1],
-                    in1=mean0_sq[:, 0:n], op0=ALU.mult, op1=ALU.subtract,
+                    out=diff[:, rows], in0=sum_sq[:, rows], scalar=inv_sum[:, b : b + 1],
+                    in1=mean0_sq[:, rows], op0=ALU.mult, op1=ALU.subtract,
                 ),
                 lambda: nc.vector.tensor_scalar_max(
-                    out=var0[:, rows], in0=diff[:, 0:n], scalar1=EPS_STD
+                    out=var0[:, rows], in0=diff[:, rows], scalar1=EPS_STD
                 ),
             ]
 
-        def invert_mask_sum(b):
-            nc.vector.reciprocal(out=inv_sum[:, b : b + 1], in_=mask_sum[:, b : b + 1])
+        def invert_mask_sums(first, stop):
+            bs = slice(first, stop)
+            nc.vector.reciprocal(out=inv_sum[:, bs], in_=mask_sum[:, bs])
             nc.vector.tensor_scalar_mul(
-                out=inv_sum_256[:, b : b + 1], in0=inv_sum[:, b : b + 1], scalar1=256.0
+                out=inv_sum_256[:, bs], in0=inv_sum[:, bs], scalar1=256.0
             )
             nc.vector.tensor_tensor(
-                out=inv_sum_256_sq[:, b : b + 1], in0=inv_sum_256[:, b : b + 1],
-                in1=inv_sum_256[:, b : b + 1], op=ALU.mult,
+                out=inv_sum_256_sq[:, bs], in0=inv_sum_256[:, bs], in1=inv_sum_256[:, bs],
+                op=ALU.mult,
             )
 
         def square_root(b):
@@ -435,7 +460,7 @@ def tile_attentivestatspool_pa_kernel(tc, x, mask, w1, b1, g1, be1, out):
                 normed = four.tile([P, T_TILES, H], F32, tag="normed")
                 normed_out[b] = normed
             rstd, shift = scales[(b, tb)]
-            if b >= B - 2 and tb % 2 == 0:
+            if b == B - 1:
                 nc.vector.tensor_scalar(
                     out=normed_out[b][:, tb, :], in0=u_banks[(b, tb)][:],
                     scalar1=rstd, scalar2=shift,
@@ -449,7 +474,10 @@ def tile_attentivestatspool_pa_kernel(tc, x, mask, w1, b1, g1, be1, out):
 
         def finish(b, ht, blocks):
             frames = slice(P * blocks.start, P * blocks.stop)
-            back = ps_mx.tile([P, T], F32, tag="mx")
+            if b < 2:
+                back = ps_first.tile([P, T], F32, tag="first")
+            else:
+                back = ps_mx.tile([P, T], F32, tag="mx")
             for tb in blocks:
                 nc.tensor.transpose(
                     back[:, P * tb : P * (tb + 1)],
@@ -489,27 +517,26 @@ def tile_attentivestatspool_pa_kernel(tc, x, mask, w1, b1, g1, be1, out):
         channel_stats(0, 0, SLOT)
         mask_x(0, 2)
         channel_stats(0, 1, SLOT)
-        invert_mask_sum(0)
-        channel_stats(0, 2, SLOT)
-        steps = stat_steps(0, ALL)
+        invert_mask_sums(0, 1)
+        channel_stats(0, 2, range(SLOTS - SCALAR_ROWS))
         for g in ALL:
             quantise_x(0, g)
-            for step in steps[2 * g : 2 * g + 2]:
-                step()
         spread_mask(1)
         mask_x(1, 0)
-        for step in steps[6:]:
-            step()
-        mask_x(1, 1)
         for g in range(5):
             transpose_w(g)
-        for g in range(5):
+        scalar_sums(0)
+        for g in range(3):
+            quantise_w(g)
+        mask_x(1, 1)
+        for g in range(3, 5):
             quantise_w(g)
         spread_mask(2)
         for g in range(5, 7):
             transpose_w(g)
+        group_x(1, 0)
+        channel_stats(1, 0, SLOT, stat_steps(0, ALL))
         square_root(0)
-        channel_stats(1, 0, SLOT)
         for g in range(5, 7):
             quantise_w(g)
         spread_mask(3)
@@ -518,7 +545,6 @@ def tile_attentivestatspool_pa_kernel(tc, x, mask, w1, b1, g1, be1, out):
             transpose_w(g)
         param_ps = ps_mx.tile([P, P], BF16, tag="mx")
         nc.tensor.transpose(param_ps[:], param_rows[:], ident_bf16[:])
-        group_x(1, 0)
         mask_x(1, 2)
         channel_stats(1, 1, range(0, 2))
         for g in range(7, W_PASSES):
@@ -528,69 +554,75 @@ def tile_attentivestatspool_pa_kernel(tc, x, mask, w1, b1, g1, be1, out):
         stat_product(0)
         group_x(1, 1)
         channel_stats(1, 1, range(2, 4))
-        invert_mask_sum(1)
+        invert_mask_sums(1, B)
         quantise_x(1, 0)
         mask_x(2, 0)
-        bias_and_relu(0)
         group_x(1, 2)
+        scalar_sums(1)
+        bias_and_relu(0)
         for b in range(1, last):
             if b > 1:
                 mask_x(b, 2)
-                channel_stats(b, 1, range(0, 2))
                 quantise_stats(b - 1)
                 first_products(b - 1)
                 stat_product(b - 1)
-                channel_stats(b, 1, range(2, 4))
-                invert_mask_sum(b)
-                mask_x(b + 1, 0)
-                channel_stats(b, 2, range(0, 1))
-                bias_and_relu(b - 1)
+                channel_stats(b, 1, SLOT)
+                scalar_sums(b)
             quantise_x(b, 1)
+            if b > 1:
+                bias_and_relu(b - 1)
             for pair in range(2):
                 transpose_u(b - 1, pair)
             group_x(b + 1, 0)
-            channel_stats(b, 2, range(b - 1, 4))
-            mask_x(b + 1, 1)
+            if b > 1:
+                mask_x(b + 1, 0)
+            channel_stats(b, 2, range(SLOTS - SCALAR_ROWS))
             group_x(b + 1, 1)
             quantise_x(b, 2)
+            mask_x(b + 1, 1)
             frame_stats(b - 1, range(T_TILES))
             frame_deviation(b - 1, range(T_TILES))
+            group_x(b + 1, 2)
             channel_stats(b + 1, 0, SLOT, stat_steps(b, ALL))
             frame_scales(b - 1, range(T_TILES))
+            square_root(b)
             for tb in range(T_TILES):
                 normalise(b - 1, tb)
-            square_root(b)
-            group_x(b + 1, 2)
             quantise_x(b + 1, 0)
         load_tanh()
         mask_x(last, 2)
-        channel_stats(last, 1, range(0, 2))
         quantise_stats(last - 1)
         first_products(last - 1)
         stat_product(last - 1)
-        channel_stats(last, 1, range(2, 4))
-        invert_mask_sum(last)
-        quantise_x(last, 1)
-        quantise_x(last, 2)
+        channel_stats(last, 1, SLOT)
+        scalar_sums(last)
         steps = stat_steps(last, range(0, 2))
-        channel_stats(last, 2, range(0, 1), steps[0:2])
+        for step in steps[0:2]:
+            step()
+        quantise_x(last, 1)
+        for step in steps[2:4]:
+            step()
         bias_and_relu(last - 1)
+        for ht in TILES:
+            finish(0, ht, range(T_TILES))
+        for step in steps[4:6]:
+            step()
+        quantise_x(last, 2)
+        first_products(last)
         for pair in range(2):
+            finish(1, 2 * pair, range(T_TILES))
+            finish(1, 2 * pair + 1, range(T_TILES))
             transpose_u(last - 1, pair)
-        channel_stats(last, 2, range(1, 3), steps[2:8])
+        channel_stats(last, 2, range(0, 1), steps[6:8])
         power_root(last, range(0, 2))
-        channel_stats(last, 2, range(3, 4))
+        channel_stats(last, 2, range(1, SLOTS - SCALAR_ROWS))
         for step in stat_steps(last, range(2, 3)):
             step()
         power_root(last, range(2, 3))
-        for ht in TILES:
-            finish(0, ht, range(T_TILES))
-        main_product(last, range(0, 2))
         frame_stats(last - 1, range(0, 2))
         frame_root_pow(last - 1, range(0, 2))
         quantise_stats(last)
         stat_product(last)
-        main_product(last, range(2, 3))
         frame_shift(last - 1, range(0, 2))
         normalise(last - 1, 0)
         normalise(last - 1, 1)
@@ -602,8 +634,6 @@ def tile_attentivestatspool_pa_kernel(tc, x, mask, w1, b1, g1, be1, out):
         normalise(last - 1, 3)
         transpose_u(last, 0)
         transpose_u(last, 1)
-        for ht in TILES:
-            finish(1, ht, range(T_TILES))
         frame_stats(last, range(0, 2))
         frame_root_pow(last, range(0, 2))
         frame_stats(last, range(2, 4))
@@ -612,7 +642,7 @@ def tile_attentivestatspool_pa_kernel(tc, x, mask, w1, b1, g1, be1, out):
             finish(last - 1, ht, range(T_TILES))
         for pair in range(2):
             frame_shift(last, range(2 * pair, 2 * pair + 2))
-            for i in range(2):
-                normalise(last, 2 * pair + i)
+            normalise(last, 2 * pair)
+            normalise(last, 2 * pair + 1)
             for ht in TILES:
                 finish(last, ht, range(2 * pair, 2 * pair + 2))

@@ -205,9 +205,9 @@ def tile_attentivestatspool_pa_kernel(tc, x, mask, w1, b1, g1, be1, out):
             x_group = four.tile([P, T, SLOTS], BF16, tag="x_group", align_bytes=64)
             x_grouped[(b, g)] = x_group
             nc.scalar.copy(
-                out=x_group[:].rearrange("p (c i) j -> p c j i", i=4),
+                out=x_group[:].rearrange("p (c i) j -> p c j i", i=8),
                 in_=x_tiles[b][:, SLOTS * g : SLOTS * (g + 1), :].rearrange(
-                    "p j (c i) -> p c j i", i=4
+                    "p j (c i) -> p c j i", i=8
                 ),
             )
 

@@ -540,25 +540,26 @@ def tile_attentivestatspool_pa_kernel(tc, x, mask, w1, b1, g1, be1, out):
         for g in range(5, 7):
             quantise_w(g)
         spread_mask(3)
-        first_products(0)
         for g in range(7, W_PASSES):
             transpose_w(g)
         param_ps = ps_mx.tile([P, P], BF16, tag="mx")
         nc.tensor.transpose(param_ps[:], param_rows[:], ident_bf16[:])
+        first_products(0)
         mask_x(1, 2)
-        channel_stats(1, 1, range(0, 2))
+        channel_stats(1, 1, SLOT)
+        quantise_x(1, 0)
         for g in range(7, W_PASSES):
             quantise_w(g)
         nc.vector.tensor_copy(out=params[:], in_=param_ps[:, 0:12])
         quantise_stats(0)
         stat_product(0)
         group_x(1, 1)
-        channel_stats(1, 1, range(2, 4))
         invert_mask_sums(1, B)
-        quantise_x(1, 0)
         mask_x(2, 0)
+        channel_stats(1, 2, range(SLOTS - SCALAR_ROWS))
         group_x(1, 2)
         scalar_sums(1)
+        group_x(2, 0)
         bias_and_relu(0)
         for b in range(1, last):
             if b > 1:
@@ -568,27 +569,27 @@ def tile_attentivestatspool_pa_kernel(tc, x, mask, w1, b1, g1, be1, out):
                 stat_product(b - 1)
                 channel_stats(b, 1, SLOT)
                 scalar_sums(b)
-            quantise_x(b, 1)
-            if b > 1:
+                quantise_x(b, 1)
+                mask_x(b + 1, 0)
+                group_x(b + 1, 0)
                 bias_and_relu(b - 1)
+                channel_stats(b, 2, range(SLOTS - SCALAR_ROWS))
+            else:
+                quantise_x(b, 1)
             for pair in range(2):
                 transpose_u(b - 1, pair)
-            group_x(b + 1, 0)
-            if b > 1:
-                mask_x(b + 1, 0)
-            channel_stats(b, 2, range(SLOTS - SCALAR_ROWS))
             group_x(b + 1, 1)
             quantise_x(b, 2)
             mask_x(b + 1, 1)
-            frame_stats(b - 1, range(T_TILES))
-            frame_deviation(b - 1, range(T_TILES))
             group_x(b + 1, 2)
             channel_stats(b + 1, 0, SLOT, stat_steps(b, ALL))
-            frame_scales(b - 1, range(T_TILES))
             square_root(b)
+            frame_stats(b - 1, range(T_TILES))
+            frame_deviation(b - 1, range(T_TILES))
+            quantise_x(b + 1, 0)
+            frame_scales(b - 1, range(T_TILES))
             for tb in range(T_TILES):
                 normalise(b - 1, tb)
-            quantise_x(b + 1, 0)
         load_tanh()
         mask_x(last, 2)
         quantise_stats(last - 1)

@@ -63,16 +63,20 @@ def tile_attentivestatspool_pa_kernel(tc, x, mask, w1, b1, g1, be1, out):
         param_rows = const.tile([P, P], BF16)
         nc.gpsimd.memset(param_rows[:], 0.0)
 
-        def load_x(b):
-            x_tile = loads.tile([P, ROWS, T], BF16, tag="load", name="x_tile%d" % b)
-            for g in range(X_PASSES):
-                nc.sync.dma_start(
-                    out=x_tile[:, SLOTS * g : SLOTS * (g + 1), :],
-                    in_=x[b, K_PASS * g : K_PASS * (g + 1), :].rearrange(
-                        "(p j) t -> p j t", j=SLOTS
-                    ),
-                )
-            return x_tile
+        x_tiles = {}
+
+        def load_x(b, passes):
+            if 0 in passes:
+                x_tile = loads.tile([P, ROWS, T], BF16, tag="load", name="x_tile%d" % b)
+                x_tiles[b] = x_tile
+            for g in passes:
+                load_x_pass(b, g)
+
+        def load_x_pass(b, g):
+            nc.sync.dma_start(
+                out=x_tiles[b][:, SLOTS * g : SLOTS * (g + 1), :],
+                in_=x[b, K_PASS * g : K_PASS * (g + 1), :].rearrange("(p j) t -> p j t", j=SLOTS),
+            )
 
         def load_w(third):
             w_tile = loads.tile([P, H_TILES, C], BF16, tag="load", name="w_tile%d" % third)
@@ -82,15 +86,17 @@ def tile_attentivestatspool_pa_kernel(tc, x, mask, w1, b1, g1, be1, out):
             )
             return w_tile
 
-        x_tiles = [load_x(0)]
+        load_x(0, range(X_PASSES))
         nc.sync.dma_start(out=mask_row[0:1, T : B * T], in_=mask_flat[:, T : B * T])
-        w_tiles = [load_w(third) for third in range(3)]
-        x_tiles.append(load_x(1))
+        w_tiles = [load_w(0), load_w(1)]
+        load_x(1, range(0, 1))
+        w_tiles.append(load_w(2))
+        load_x(1, range(1, X_PASSES))
         nc.sync.dma_start(out=param_rows[0:4, :], in_=b1.rearrange("(r c) -> r c", c=P))
         nc.sync.dma_start(out=param_rows[4:8, :], in_=g1.rearrange("(r c) -> r c", c=P))
         nc.sync.dma_start(out=param_rows[8:12, :], in_=be1.rearrange("(r c) -> r c", c=P))
-        x_tiles.append(load_x(2))
-        x_tiles.append(load_x(3))
+        load_x(2, range(X_PASSES))
+        load_x(3, range(X_PASSES))
 
         ident_f32 = const.tile([P, P], F32)
         make_identity(nc, ident_f32[:])
@@ -603,33 +609,36 @@ def tile_attentivestatspool_pa_kernel(tc, x, mask, w1, b1, g1, be1, out):
         quantise_x(last, 1)
         for step in steps[2:4]:
             step()
-        bias_and_relu(last - 1)
-        for ht in TILES:
-            finish(0, ht, range(T_TILES))
+        quantise_x(last, 2)
         for step in steps[4:6]:
             step()
-        quantise_x(last, 2)
-        first_products(last)
-        for pair in range(2):
-            finish(1, 2 * pair, range(T_TILES))
-            finish(1, 2 * pair + 1, range(T_TILES))
-            transpose_u(last - 1, pair)
-        channel_stats(last, 2, range(0, 1), steps[6:8])
+        bias_and_relu(last - 1)
+        for step in steps[6:8]:
+            step()
         power_root(last, range(0, 2))
-        channel_stats(last, 2, range(1, SLOTS - SCALAR_ROWS))
+        for ht in TILES:
+            finish(0, ht, range(T_TILES))
+        first_products(last)
+        finish(1, 0, range(T_TILES))
+        finish(1, 1, range(T_TILES))
+        transpose_u(last - 1, 0)
+        channel_stats(last, 2, range(SLOTS - SCALAR_ROWS))
         for step in stat_steps(last, range(2, 3)):
             step()
         power_root(last, range(2, 3))
-        frame_stats(last - 1, range(0, 2))
-        frame_root_pow(last - 1, range(0, 2))
         quantise_stats(last)
         stat_product(last)
+        finish(1, 2, range(T_TILES))
+        finish(1, 3, range(T_TILES))
+        transpose_u(last - 1, 1)
+        frame_stats(last - 1, range(0, 2))
+        frame_root_pow(last - 1, range(0, 2))
         frame_shift(last - 1, range(0, 2))
         normalise(last - 1, 0)
         normalise(last - 1, 1)
+        bias_and_relu(last)
         frame_stats(last - 1, range(2, 4))
         frame_root_pow(last - 1, range(2, 4))
-        bias_and_relu(last)
         frame_shift(last - 1, range(2, 4))
         normalise(last - 1, 2)
         normalise(last - 1, 3)

from contextlib import ExitStack

import concourse.mybir as mybir
from concourse.masks import make_identity

F32 = mybir.dt.float32
BF16 = mybir.dt.bfloat16
U32 = mybir.dt.uint32
U8 = mybir.dt.uint8
FP8X4 = mybir.dt.float8_e4m3fn_x4
ALU = mybir.AluOpType
ACT = mybir.ActivationFunctionType
AX = mybir.AxisListType

B, C, T, H = 4, 1536, 512, 512
P = 128
SLOTS = 4
K_PASS = P * SLOTS
X_PASSES = C // K_PASS
W_PASSES = 3 * X_PASSES
ROWS = X_PASSES * SLOTS
H_TILES = H // P
T_TILES = T // P
SCALAR_ROWS = 2
STAT_STEP = 64
EPS_LN = 1e-5
EPS_STD = 1e-5
FLOPS = 2 * B * H * 3 * C * T


def tile_attentivestatspool_pa_kernel(tc, x, mask, w1, b1, g1, be1, out):
    nc = tc.nc
    with ExitStack() as ctx:
        const = ctx.enter_context(tc.tile_pool(name="const", bufs=1))
        loads = ctx.enter_context(tc.tile_pool(name="loads", bufs=6))
        five = ctx.enter_context(tc.tile_pool(name="five", bufs=5))
        four = ctx.enter_context(tc.tile_pool(name="four", bufs=4))
        two = ctx.enter_context(tc.tile_pool(name="two", bufs=2))
        ps_first = ctx.enter_context(tc.psum_pool(name="ps_first", bufs=4))
        ps_mx = ctx.enter_context(tc.psum_pool(name="ps_mx", bufs=4))
        ctx.enter_context(
            tc.manual_schedule(
                engines={
                    mybir.EngineType.DVE, mybir.EngineType.Activation,
                    mybir.EngineType.PE, mybir.EngineType.Pool,
                }
            )
        )

        mask_row = const.tile([P, B * T], BF16)
        mask_words = mask_row[:].bitcast(F32)
        nc.vector.memset(mask_words[:, 0 : T // 2], 0.0)
        nc.gpsimd.memset(mask_words[:, T // 2 : B * T // 2], 0.0)
        mask_flat = mask.rearrange("b o t -> o (b t)")
        nc.sync.dma_start(out=mask_row[0:1, 0:T], in_=mask_flat[:, 0:T])
        ones = const.tile([P, P], BF16)
        nc.vector.memset(ones[:], 1.0)
        mask_all = const.tile([P, B, T], BF16)
        mask_sum = const.tile([P, B], F32)
        warm = const.tile([P, 1], F32)
        nc.vector.memset(warm[:], 1.0)
        nc.scalar.activation(out=warm[:], in_=warm[:], func=ACT.Sqrt)
        param_rows = const.tile([P, P], BF16)
        nc.gpsimd.memset(param_rows[:], 0.0)

        x_tiles = {}

        def load_x(b, passes):
            if 0 in passes:
                x_tile = loads.tile([P, ROWS, T], BF16, tag="load", name="x_tile%d" % b)
                x_tiles[b] = x_tile
            for g in passes:
                load_x_pass(b, g)

        def load_x_pass(b, g):
            nc.sync.dma_start(
                out=x_tiles[b][:, SLOTS * g : SLOTS * (g + 1), :],
                in_=x[b, K_PASS * g : K_PASS * (g + 1), :].rearrange("(p j) t -> p j t", j=SLOTS),
            )

        def load_w(third):
            w_tile = loads.tile([P, H_TILES, C], BF16, tag="load", name="w_tile%d" % third)
            nc.sync.dma_start(
                out=w_tile[:],
                in_=w1[:, C * third : C * (third + 1)].rearrange("(a p) k -> p a k", p=P),
            )
            return w_tile

        load_x(0, range(X_PASSES))
        nc.sync.dma_start(out=mask_row[0:1, T : B * T], in_=mask_flat[:, T : B * T])
        w_tiles = [load_w(0), load_w(1)]
        load_x(1, range(0, 1))
        w_tiles.append(load_w(2))
        load_x(1, range(1, X_PASSES))
        nc.sync.dma_start(out=param_rows[0:4, :], in_=b1.rearrange("(r c) -> r c", c=P))
        nc.sync.dma_start(out=param_rows[4:8, :], in_=g1.rearrange("(r c) -> r c", c=P))
        nc.sync.dma_start(out=param_rows[8:12, :], in_=be1.rearrange("(r c) -> r c", c=P))
        load_x(2, range(X_PASSES))
        load_x(3, range(X_PASSES))

        ident_f32 = const.tile([P, P], F32)
        make_identity(nc, ident_f32[:])
        ident_bf16 = const.tile([P, P], BF16)
        make_identity(nc, ident_bf16[:])
        stat_in = const.tile([P, 8, STAT_STEP, SLOTS], BF16, align_bytes=64)
        nc.gpsimd.memset(stat_in[:].rearrange("p s n j -> p (s n j)").bitcast(F32), 0.0)
        half = const.tile([P, X_PASSES, SLOTS], F32)
        nc.gpsimd.memset(half[:], 0.5)
        eps_ln = const.tile([P, 1], F32)
        nc.vector.memset(eps_ln[:], 0.0)
        nc.vector.tensor_scalar_add(out=eps_ln[:], in0=eps_ln[:], scalar1=EPS_LN)
        minus_half = const.tile([P, 4], F32)
        nc.gpsimd.memset(minus_half[:], -0.5)

        w_codes = const.tile([P, W_PASSES, H], U32, align_bytes=64)
        w_scales = const.tile([P, W_PASSES, H], U8, align_bytes=64)

        def spread_mask(b):
            mask_ps = ps_mx.tile([P, T], F32, tag="mx")
            nc.tensor.matmul(
                out=mask_ps[:], lhsT=ones[:], rhs=mask_row[:, T * b : T * (b + 1)],
                start=True, stop=True,
            )
            if b == 0:
                nc.vector.tensor_scalar(
                    out=mask_all[:, b, :], in0=mask_ps[:], scalar1=1.0, scalar2=0.0,
                    op0=ALU.mult, op1=ALU.add, accum_out=mask_sum[:, b : b + 1],
                )
            else:
                nc.scalar.activation(
                    out=mask_all[:, b, :], in_=mask_ps[:], func=ACT.Copy,
                    accum_out=mask_sum[:, b : b + 1],
                )
        inv_sum = const.tile([P, B], F32)
        inv_sum_256 = const.tile([P, B], F32)
        inv_sum_256_sq = const.tile([P, B], F32)
        params = const.tile([P, 12], F32)

        masked = {}
        stats = {}
        sums = {}
        variances = {}
        x_grouped = {}
        x_quant = {}
        w_grouped = {}
        stat_quant = {}
        stat_ps = {}
        main_ps = {}
        results = {}
        biases = {}
        relu_out = {}
        u_banks = {}
        frame_moments = {}
        roots = {}
        deviations = {}
        scales = {}
        normed_out = {}

        def mask_x(b, g):
            x_masked = two.tile([P, SLOTS, T], BF16, tag="x_masked")
            masked[(b, g)] = x_masked
            nc.vector.tensor_tensor(
                out=x_masked[:],
                in0=x_tiles[b][:, SLOTS * g : SLOTS * (g + 1), :],
                in1=mask_all[:, b, :].unsqueeze(1).to_broadcast([P, SLOTS, T]),
                op=ALU.mult,
            )

        def channel_stats(b, g, slots, between=()):
            if g == 0 and slots.start == 0:
                stats_b = two.tile([P, ROWS, 6], F32, tag="stats")
                stats[b] = stats_b
            for n, j in enumerate(slots):
                nc.vector.bn_stats(
                    out=stats[b][:, SLOTS * g + j, :], in_=masked[(b, g)][:, j, :]
                )
                for step in between[2 * n : 2 * n + 2]:
                    step()
            for step in between[2 * len(slots) :]:
                step()

        def transpose_w(g):
            third, g_in = divmod(g, X_PASSES)
            w_words = w_tiles[third][:].bitcast(F32)
            w_group = five.tile([P, H, SLOTS], BF16, tag="w_group", align_bytes=64)
            w_grouped[g] = w_group
            group_words = w_group[:].bitcast(F32)
            for pair in range(2):
                w_ps = ps_first.tile([P, 2, 2 * P], F32, tag="first")
                for u in range(2):
                    for a in range(2):
                        first_word = 2 * P * g_in + u
                        nc.tensor.transpose(
                            w_ps[:, u, P * a : P * (a + 1)],
                            w_words[:, 2 * pair + a, first_word : first_word + 2 * P - 1 : 2],
                            ident_f32[:],
                        )
                nc.scalar.copy(
                    out=group_words[:, 2 * P * pair : 2 * P * (pair + 1), :],
                    in_=w_ps[:].rearrange("p u n -> p n u"),
                )

        def quantise_w(g):
            nc.vector.quantize_mx(
                out=w_codes[:, g, :].bitcast(FP8X4),
                scales=w_scales[:, g, :],
                in_=w_grouped[g][:].rearrange("p h j -> p (h j)"),
            )

        def group_x(b, g):
            x_group = four.tile([P, T, SLOTS], BF16, tag="x_group", align_bytes=64)
            x_grouped[(b, g)] = x_group
            nc.scalar.copy(
                out=x_group[:].rearrange("p (c i) j -> p c j i", i=8),
                in_=x_tiles[b][:, SLOTS * g : SLOTS * (g + 1), :].rearrange(
                    "p j (c i) -> p c j i", i=8
                ),
            )

        def quantise_x(b, g):
            if g == 0:
                x_codes = two.tile([P, X_PASSES, T], U32, tag="x_codes", align_bytes=64)
                x_scales = two.tile([P, X_PASSES, T], U8, tag="x_scales", align_bytes=64)
                x_quant[b] = (x_codes, x_scales)
            x_codes, x_scales = x_quant[b]
            nc.vector.quantize_mx(
                out=x_codes[:, g, :].bitcast(FP8X4),
                scales=x_scales[:, g, :],
                in_=x_grouped[(b, g)][:].rearrange("p t j -> p (t j)"),
            )

        def new_sums(b):
            sum_x = two.tile([P, ROWS], F32, tag="sum_x")
            sum_sq = two.tile([P, ROWS], F32, tag="sum_sq")
            sums[b] = (sum_x, sum_sq)

        def scalar_sums(b):
            new_sums(b)
            sum_x, sum_sq = sums[b]
            for row in range(ROWS - SCALAR_ROWS, ROWS):
                channel = masked[(b, X_PASSES - 1)][:, row % SLOTS, :]
                unused = two.tile([P, T], BF16, tag="unused")
                nc.scalar.activation(
                    out=unused[:], in_=channel, func=ACT.Identity, scale=1.0 / 256.0,
                    accum_out=sum_x[:, row : row + 1],
                )
                unused = two.tile([P, T], BF16, tag="unused")
                nc.scalar.activation(
                    out=unused[:], in_=channel, func=ACT.Square,
                    accum_out=sum_sq[:, row : row + 1],
                )

        def stat_steps(b, groups):
            rows = slice(SLOTS * groups.start, SLOTS * groups.stop)
            if groups.start == 0:
                var0 = two.tile([P, ROWS], F32, tag="var0")
                variances[b] = var0
            if b not in sums:
                new_sums(b)
            var0 = variances[b]
            sum_x, sum_sq = sums[b]
            seen = slice(rows.start, min(rows.stop, ROWS - SCALAR_ROWS))
            half_mean = stats[b][:, seen, :].rearrange("p r (h s) -> p r h s", s=3)[:, :, :, 1]
            half_dev = stats[b][:, seen, :].rearrange("p r (h s) -> p r h s", s=3)[:, :, :, 2]
            mean_sq = two.tile([P, ROWS, 2], F32, tag="mean_sq")
            half_sq = two.tile([P, ROWS, 2], F32, tag="half_sq")
            mean0_sq = two.tile([P, ROWS], F32, tag="mean0_sq")
            diff = two.tile([P, ROWS], F32, tag="diff")
            return [
                lambda: nc.vector.tensor_tensor(
                    out=mean_sq[:, seen, :], in0=half_mean, in1=half_mean, op=ALU.mult
                ),
                lambda: nc.vector.tensor_tensor(
                    out=sum_x[:, seen], in0=half_mean[:, :, 0], in1=half_mean[:, :, 1],
                    op=ALU.add,
                ),
                lambda: nc.vector.scalar_tensor_tensor(
                    out=half_sq[:, seen, :], in0=mean_sq[:, seen, :], scalar=256.0, in1=half_dev,
                    op0=ALU.mult, op1=ALU.add,
                ),
                lambda: nc.vector.scalar_tensor_tensor(
                    out=mean0_sq[:, rows], in0=sum_x[:, rows],
                    scalar=inv_sum_256_sq[:, b : b + 1], in1=sum_x[:, rows],
                    op0=ALU.mult, op1=ALU.mult,
                ),
                lambda: nc.vector.tensor_tensor(
                    out=sum_sq[:, seen], in0=half_sq[:, seen, 0], in1=half_sq[:, seen, 1],
                    op=ALU.add,
                ),
                lambda: nc.vector.tensor_scalar_mul(
                    out=stat_in[:, groups.start : groups.stop, b, :],
                    in0=sum_x[:, rows].rearrange("p (g j) -> p g j", j=SLOTS),
                    scalar1=inv_sum_256[:, b : b + 1],
                ),
                lambda: nc.vector.scalar_tensor_tensor(
                    out=diff[:, rows], in0=sum_sq[:, rows], scalar=inv_sum[:, b : b + 1],
                    in1=mean0_sq[:, rows], op0=ALU.mult, op1=ALU.subtract,
                ),
                lambda: nc.vector.tensor_scalar_max(
                    out=var0[:, rows], in0=diff[:, rows], scalar1=EPS_STD
                ),
            ]

        def invert_mask_sums(first, stop):
            bs = slice(first, stop)
            nc.vector.reciprocal(out=inv_sum[:, bs], in_=mask_sum[:, bs])
            nc.vector.tensor_scalar_mul(
                out=inv_sum_256[:, bs], in0=inv_sum[:, bs], scalar1=256.0
            )
            nc.vector.tensor_tensor(
                out=inv_sum_256_sq[:, bs], in0=inv_sum_256[:, bs], in1=inv_sum_256[:, bs],
                op=ALU.mult,
            )

        def square_root(b):
            nc.scalar.activation(
                out=stat_in[:, X_PASSES : 2 * X_PASSES, b, :], in_=variances[b][:].rearrange(
                    "p (g j) -> p g j", j=SLOTS
                ), func=ACT.Sqrt
            )

        def load_tanh():
            nc.scalar.activation(out=warm[:], in_=warm[:], func=ACT.Tanh)

        def power_root(b, groups):
            gs = slice(groups.start, groups.stop)
            n = len(groups)
            nc.gpsimd.tensor_tensor(
                out=stat_in[:, X_PASSES + groups.start : X_PASSES + groups.stop, b, :],
                in0=variances[b][:].rearrange("p (g j) -> p g j", j=SLOTS)[:, gs, :],
                in1=half[:, 0:n, :], op=ALU.pow,
            )

        def quantise_stats(b):
            stat_codes = two.tile([P, 8 * STAT_STEP], U32, tag="stat_codes", align_bytes=64)
            stat_scales = two.tile([P, 8 * STAT_STEP], U8, tag="stat_scales", align_bytes=64)
            nc.vector.quantize_mx(
                out=stat_codes[:].bitcast(FP8X4),
                scales=stat_scales[:],
                in_=stat_in[:].rearrange("p s n j -> p (s n j)"),
            )
            stat_quant[b] = (stat_codes, stat_scales)

        def stat_product(b):
            stat_codes, stat_scales = stat_quant[b]
            product = ps_mx.tile([P, H_TILES, P], F32, tag="mx")
            stat_ps[b] = product
            for ht in range(H_TILES):
                for s in range(2 * X_PASSES):
                    nc.tensor.matmul_mx(
                        out=product[:, ht, :],
                        lhsT=w_codes[:, X_PASSES + s, P * ht : P * (ht + 1)].bitcast(FP8X4),
                        lhsT_scale=w_scales[:, X_PASSES + s, P * ht : P * (ht + 1)],
                        rhs=stat_codes[:, STAT_STEP * s : STAT_STEP * s + P].bitcast(FP8X4),
                        rhs_scale=stat_scales[:, STAT_STEP * s : STAT_STEP * s + P],
                        start=(s == 0),
                        stop=(s == 2 * X_PASSES - 1),
                    )

        def main_product(b, h_tiles):
            x_codes, x_scales = x_quant[b]
            if 0 in h_tiles:
                main_ps[b] = []
            for ht in h_tiles:
                acc = ps_mx.tile([P, T], F32, tag="mx")
                main_ps[b].append(acc)
                for g in range(X_PASSES):
                    nc.tensor.matmul_mx(
                        out=acc[:],
                        lhsT=w_codes[:, g, P * ht : P * (ht + 1)].bitcast(FP8X4),
                        lhsT_scale=w_scales[:, g, P * ht : P * (ht + 1)],
                        rhs=x_codes[:, g, :].bitcast(FP8X4),
                        rhs_scale=x_scales[:, g, :],
                        start=(g == 0),
                        stop=(g == X_PASSES - 1),
                    )

        def add_bias(b):
            bias = two.tile([P, H_TILES], F32, tag="bias")
            biases[b] = bias
            nc.vector.tensor_tensor(
                out=bias[:], in0=stat_ps[b][:, :, b], in1=params[:, 0:4], op=ALU.add
            )

        def relu(b, ht):
            if ht == 0:
                u = two.tile([P, H_TILES, T], F32, tag="u")
                relu_out[b] = u
            if b == B - 1 and ht % 2 == 0:
                nc.vector.tensor_scalar(
                    out=relu_out[b][:, ht, :], in0=main_ps[b][ht][:],
                    scalar1=biases[b][:, ht : ht + 1], scalar2=0.0, op0=ALU.add, op1=ALU.max,
                )
            else:
                nc.scalar.activation(
                    out=relu_out[b][:, ht, :], in_=main_ps[b][ht][:], func=ACT.Relu,
                    bias=biases[b][:, ht : ht + 1], scale=1.0,
                )

        def transpose_u(b, pair):
            for tb in range(2 * pair, 2 * pair + 2):
                u_t = ps_first.tile([P, H], F32, tag="first")
                u_banks[(b, tb)] = u_t
                for ht in range(H_TILES):
                    nc.tensor.transpose(
                        u_t[:, P * ht : P * (ht + 1)],
                        relu_out[b][:, ht, P * tb : P * (tb + 1)], ident_f32[:],
                    )

        def frame_stats(b, blocks):
            ln_stats = four.tile([P, T_TILES, 6], F32, tag="ln_stats")
            mean_var = four.tile([P, T_TILES, 2], F32, tag="mean_var")
            frame_moments[(b, blocks.start)] = mean_var
            for i, tb in enumerate(blocks):
                nc.vector.bn_stats(out=ln_stats[:, i, :], in_=u_banks[(b, tb)][:])
            for i in range(len(blocks)):
                nc.vector.bn_aggr(out=mean_var[:, i, :], in_=ln_stats[:, i, :])

        def frame_deviation(b, blocks):
            deviation = four.tile([P, T_TILES], F32, tag="deviation")
            deviations[b] = deviation
            nc.scalar.activation(
                out=deviation[:], in_=frame_moments[(b, blocks.start)][:, :, 1], func=ACT.Sqrt,
                bias=eps_ln[:],
            )

        def frame_scales(b, blocks):
            mean_var = frame_moments[(b, blocks.start)]
            rstd = four.tile([P, T_TILES], F32, tag="rstd")
            nc.vector.reciprocal(out=rstd[:], in_=deviations[b][:])
            shift = four.tile([P, T_TILES], F32, tag="shift")
            nc.vector.scalar_tensor_tensor(
                out=shift[:], in0=mean_var[:, :, 0], scalar=-1.0, in1=rstd[:],
                op0=ALU.mult, op1=ALU.mult,
            )
            for i, tb in enumerate(blocks):
                scales[(b, tb)] = (rstd[:, i : i + 1], shift[:, i : i + 1])

        def frame_root_pow(b, blocks):
            n = len(blocks)
            mean_var = frame_moments[(b, blocks.start)]
            var_eps = four.tile([P, T_TILES], F32, tag="var_eps")
            nc.vector.tensor_scalar_add(
                out=var_eps[:, 0:n], in0=mean_var[:, 0:n, 1], scalar1=EPS_LN
            )
            rstd = four.tile([P, T_TILES], F32, tag="rstd")
            roots[(b, blocks.start)] = rstd
            nc.gpsimd.tensor_tensor(
                out=rstd[:, 0:n], in0=var_eps[:, 0:n], in1=minus_half[:, 0:n], op=ALU.pow
            )

        def frame_shift(b, blocks):
            n = len(blocks)
            mean_var = frame_moments[(b, blocks.start)]
            rstd = roots[(b, blocks.start)]
            shift = four.tile([P, T_TILES], F32, tag="shift")
            nc.vector.scalar_tensor_tensor(
                out=shift[:, 0:n], in0=mean_var[:, 0:n, 0], scalar=-1.0, in1=rstd[:, 0:n],
                op0=ALU.mult, op1=ALU.mult,
            )
            for i, tb in enumerate(blocks):
                scales[(b, tb)] = (rstd[:, i : i + 1], shift[:, i : i + 1])

        def normalise(b, tb):
            if tb == 0:
                normed = four.tile([P, T_TILES, H], F32, tag="normed")
                normed_out[b] = normed
            rstd, shift = scales[(b, tb)]
            if b == B - 1:
                nc.vector.tensor_scalar(
                    out=normed_out[b][:, tb, :], in0=u_banks[(b, tb)][:],
                    scalar1=rstd, scalar2=shift,
                    op0=ALU.mult, op1=ALU.add,
                )
            else:
                nc.scalar.activation(
                    out=normed_out[b][:, tb, :], in_=u_banks[(b, tb)][:], func=ACT.Identity,
                    scale=rstd, bias=shift,
                )

        def finish(b, ht, blocks):
            frames = slice(P * blocks.start, P * blocks.stop)
            if b < 2:
                back = ps_first.tile([P, T], F32, tag="first")
            else:
                back = ps_mx.tile([P, T], F32, tag="mx")
            for tb in blocks:
                nc.tensor.transpose(
                    back[:, P * tb : P * (tb + 1)],
                    normed_out[b][:, tb, P * ht : P * (ht + 1)],
                    ident_f32[:],
                )
            if blocks.start == 0:
                result = five.tile([P, T], F32, tag="result")
                results[(b, ht)] = result
            result = results[(b, ht)]
            nc.scalar.activation(
                out=result[:, frames], in_=back[:, frames], func=ACT.Tanh,
                scale=params[:, 4 + ht : 5 + ht], bias=params[:, 8 + ht : 9 + ht],
            )
            nc.sync.dma_start(out=out[b, P * ht : P * (ht + 1), frames], in_=result[:, frames])

        TILES = range(H_TILES)
        SLOT = range(SLOTS)
        ALL = range(X_PASSES)
        last = B - 1

        def first_products(b):
            main_product(b, range(3))

        def bias_and_relu(b):
            add_bias(b)
            for ht in TILES:
                if ht == 3:
                    main_product(b, range(3, 4))
                relu(b, ht)

        spread_mask(0)
        for g in ALL:
            group_x(0, g)
        mask_x(0, 0)
        mask_x(0, 1)
        channel_stats(0, 0, SLOT)
        mask_x(0, 2)
        channel_stats(0, 1, SLOT)
        invert_mask_sums(0, 1)
        channel_stats(0, 2, range(SLOTS - SCALAR_ROWS))
        for g in ALL:
            quantise_x(0, g)
        spread_mask(1)
        mask_x(1, 0)
        for g in range(5):
            transpose_w(g)
        scalar_sums(0)
        for g in range(3):
            quantise_w(g)
        mask_x(1, 1)
        for g in range(3, 5):
            quantise_w(g)
        spread_mask(2)
        for g in range(5, 7):
            transpose_w(g)
        group_x(1, 0)
        channel_stats(1, 0, SLOT, stat_steps(0, ALL))
        square_root(0)
        for g in range(5, 7):
            quantise_w(g)
        spread_mask(3)
        for g in range(7, W_PASSES):
            transpose_w(g)
        param_ps = ps_mx.tile([P, P], BF16, tag="mx")
        nc.tensor.transpose(param_ps[:], param_rows[:], ident_bf16[:])
        first_products(0)
        mask_x(1, 2)
        channel_stats(1, 1, SLOT)
        quantise_x(1, 0)
        for g in range(7, W_PASSES):
            quantise_w(g)
        nc.vector.tensor_copy(out=params[:], in_=param_ps[:, 0:12])
        quantise_stats(0)
        stat_product(0)
        group_x(1, 1)
        invert_mask_sums(1, B)
        mask_x(2, 0)
        channel_stats(1, 2, range(SLOTS - SCALAR_ROWS))
        group_x(1, 2)
        scalar_sums(1)
        group_x(2, 0)
        bias_and_relu(0)
        for b in range(1, last):
            if b > 1:
                mask_x(b, 2)
                quantise_stats(b - 1)
                first_products(b - 1)
                stat_product(b - 1)
                channel_stats(b, 1, SLOT)
                scalar_sums(b)
                quantise_x(b, 1)
                mask_x(b + 1, 0)
                group_x(b + 1, 0)
                bias_and_relu(b - 1)
                channel_stats(b, 2, range(SLOTS - SCALAR_ROWS))
            else:
                quantise_x(b, 1)
            for pair in range(2):
                transpose_u(b - 1, pair)
            group_x(b + 1, 1)
            quantise_x(b, 2)
            mask_x(b + 1, 1)
            group_x(b + 1, 2)
            channel_stats(b + 1, 0, SLOT, stat_steps(b, ALL))
            square_root(b)
            frame_stats(b - 1, range(T_TILES))
            frame_deviation(b - 1, range(T_TILES))
            quantise_x(b + 1, 0)
            frame_scales(b - 1, range(T_TILES))
            for tb in range(T_TILES):
                normalise(b - 1, tb)
        load_tanh()
        mask_x(last, 2)
        quantise_stats(last - 1)
        first_products(last - 1)
        stat_product(last - 1)
        channel_stats(last, 1, SLOT)
        scalar_sums(last)
        steps = stat_steps(last, range(0, 2))
        for step in steps[0:2]:
            step()
        quantise_x(last, 1)
        for step in steps[2:4]:
            step()
        quantise_x(last, 2)
        for step in steps[4:6]:
            step()
        bias_and_relu(last - 1)
        for step in steps[6:8]:
            step()
        power_root(last, range(0, 2))
        for ht in TILES:
            finish(0, ht, range(T_TILES))
        first_products(last)
        finish(1, 0, range(T_TILES))
        finish(1, 1, range(T_TILES))
        transpose_u(last - 1, 0)
        channel_stats(last, 2, range(SLOTS - SCALAR_ROWS))
        for step in stat_steps(last, range(2, 3)):
            step()
        power_root(last, range(2, 3))
        quantise_stats(last)
        stat_product(last)
        finish(1, 2, range(T_TILES))
        finish(1, 3, range(T_TILES))
        transpose_u(last - 1, 1)
        frame_stats(last - 1, range(0, 2))
        frame_root_pow(last - 1, range(0, 2))
        frame_shift(last - 1, range(0, 2))
        normalise(last - 1, 0)
        normalise(last - 1, 1)
        bias_and_relu(last)
        frame_stats(last - 1, range(2, 4))
        frame_root_pow(last - 1, range(2, 4))
        frame_shift(last - 1, range(2, 4))
        normalise(last - 1, 2)
        normalise(last - 1, 3)
        transpose_u(last, 0)
        transpose_u(last, 1)
        frame_stats(last, range(0, 2))
        frame_root_pow(last, range(0, 2))
        frame_stats(last, range(2, 4))
        frame_root_pow(last, range(2, 4))
        for ht in TILES:
            finish(last - 1, ht, range(T_TILES))
        for pair in range(2):
            frame_shift(last, range(2 * pair, 2 * pair + 2))
            normalise(last, 2 * pair)
            normalise(last, 2 * pair + 1)
            for ht in TILES:
                finish(last, ht, range(2 * pair, 2 * pair + 2))
